import numpy as np
import ml_dtypes


def mxq(x, axis, fmt="e4m3"):
    dtype, down = {"e4m3": (ml_dtypes.float8_e4m3fn, 7), "e5m2": (ml_dtypes.float8_e5m2, 14)}[fmt]
    v = np.moveaxis(np.asarray(x, np.float32).astype(ml_dtypes.bfloat16).astype(np.float64), axis, -1)
    blocks = v.reshape(v.shape[:-1] + (-1, 32))
    amax = np.abs(blocks).max(-1, keepdims=True)
    byte = np.maximum(np.where(amax > 0, np.frexp(amax)[1] - 1 + 127, 0) - down, 1)
    scale = np.exp2(byte - 127.0)
    codes = (blocks / scale).astype(np.float32).astype(dtype).astype(np.float64)
    return np.moveaxis((codes * scale).reshape(v.shape), -1, axis)


WIDE = False


def mx_kscale(k):
    if not WIDE:
        return np.ones(k)
    levels = np.array([10, -10, 5, -5, 0])
    a = np.random.permutation(np.resize(levels, k // 512 * 4)).reshape(k // 512, 4)
    idx = np.arange(k)
    return np.exp2(a[idx // 512, idx % 128 // 32])


BF16 = ml_dtypes.bfloat16


def bf(x):
    return np.asarray(x, np.float32).astype(BF16)


def f64(x):
    return np.asarray(x).astype(np.float64)


B, H, W, C, K = 1, 64, 64, 256, 2
WH, WW = H // K, W // K
WIN = WH * WW


def _split_feature(x, num_splits):
    b, hh, ww, c = x.shape
    x = x.reshape(b, num_splits, hh // num_splits, num_splits, ww // num_splits, c)
    x = x.transpose(0, 1, 3, 2, 4, 5)
    return x.reshape(b * num_splits * num_splits, hh // num_splits, ww // num_splits, c)


def _merge_splits(x, num_splits, b):
    _, hk, wk, c = x.shape
    x = x.reshape(b, num_splits, num_splits, hk, wk, c)
    x = x.transpose(0, 1, 3, 2, 4, 5)
    return x.reshape(b, num_splits * hk, num_splits * wk, c)


def setup_inputs():
    s = mx_kscale(WIN)
    smap = np.roll(np.tile(s.reshape(WH, WW), (K, K)), (WH // 2, WW // 2), axis=(0, 1)).reshape(1, H * W, 1)
    m = np.random.uniform(size=(K * K, WIN, WIN))
    noise = np.random.standard_normal((K * K, WIN, WIN)) * 0.5
    return {"q": bf(np.random.standard_normal((B, H * W, C)) * 1.4),
            "k": bf(np.random.standard_normal((B, H * W, C)) * 1.4),
            "v": bf(np.random.standard_normal((B, H * W, C)) * 2.0 * s.mean() / smap),
            "attn_mask": bf(np.where(m < 0.9, 0.0, -100.0) + noise + np.log(s)[None, None, :]),
            "num_splits": K, "with_shift": 1, "h": H, "w": W}


def reference(q, k, v, attn_mask, num_splits, with_shift, h, w):
    q, k, v, attn_mask = f64(q), f64(k), f64(v), f64(attn_mask)
    b, hw, c = q.shape
    assert hw == h * w
    q = q.reshape(b, h, w, c)
    k = k.reshape(b, h, w, c)
    v = v.reshape(b, h, w, c)
    win_h = h // num_splits
    win_w = w // num_splits
    scale = c ** 0.5
    if with_shift:
        sh, sw = win_h // 2, win_w // 2
        q = np.roll(q, (-sh, -sw), axis=(1, 2))
        k = np.roll(k, (-sh, -sw), axis=(1, 2))
        v = np.roll(v, (-sh, -sw), axis=(1, 2))
    kk = num_splits * num_splits
    L = win_h * win_w
    qs = _split_feature(q, num_splits).reshape(b * kk, L, c)
    ks = _split_feature(k, num_splits).reshape(b * kk, L, c)
    vs = _split_feature(v, num_splits).reshape(b * kk, L, c)
    scores = qs @ ks.transpose(0, 2, 1) / scale
    if with_shift:
        scores = (scores.reshape(b, kk, L, L) + attn_mask[None]).reshape(b * kk, L, L)
    e = np.exp(scores - scores.max(-1, keepdims=True))
    out = (mxq(e, 2, "e4m3") @ mxq(vs, 1, "e4m3")) / e.sum(-1, keepdims=True)
    out = _merge_splits(out.reshape(b * kk, win_h, win_w, c), num_splits, b)
    if with_shift:
        out = np.roll(out, (sh, sw), axis=(1, 2))
    return out.reshape(b, h * w, c)

@@ -1,0 +1,235 @@
+from contextlib import ExitStack
+
+import concourse.mybir as mybir
+from concourse.masks import make_identity
+
+FLOPS = 2 * 2 * 4 * 1024 * 1024 * 256
+
+F32 = mybir.dt.float32
+BF16 = mybir.dt.bfloat16
+U32 = mybir.dt.uint32
+U8 = mybir.dt.uint8
+FP8X4 = mybir.dt.float8_e4m3fn_x4
+ALU = mybir.AluOpType
+ACT = mybir.ActivationFunctionType
+AX = mybir.AxisListType
+
+P = 128
+C = 256
+NWIN = 4
+NBLK = 8
+L = 1024
+
+
+def image_block(win, blk):
+    wy, wx = divmod(win, 2)
+    yh, xo = divmod(blk, 4)
+    return (2 * wy + yh + 1) % 4, (4 * wx + xo + 2) % 8
+
+
+def tile_single_head_split_window_attention_t_kernel(
+    tc, q, k, v, attn_mask, num_splits, with_shift, h, w, out
+):
+    nc = tc.nc
+    assert (num_splits, with_shift, h, w) == (2, 1, 64, 64)
+    blocks = "o (yq rr xo xi) c -> o yq xo rr xi c"
+    q_blk = q.rearrange(blocks, yq=4, rr=16, xo=8, xi=8)
+    k_blk = k.rearrange(blocks, yq=4, rr=16, xo=8, xi=8)
+    v_blk = v.rearrange(blocks, yq=4, rr=16, xo=8, xi=8)
+    o_blk = out.rearrange(blocks, yq=4, rr=16, xo=8, xi=8)
+    m_blk = attn_mask.rearrange("j (yh rr xo xi) n -> j yh xo rr xi n", yh=2, rr=16, xo=4, xi=8)
+
+    with ExitStack() as ctx:
+        res = ctx.enter_context(tc.tile_pool(name="res", bufs=1))
+        work = ctx.enter_context(tc.tile_pool(name="work", bufs=3))
+        stat = ctx.enter_context(tc.tile_pool(name="stat", bufs=4))
+        ps_s = ctx.enter_context(tc.psum_pool(name="ps_s", bufs=2))
+        ps_e = ctx.enter_context(tc.psum_pool(name="ps_e", bufs=2))
+        ps_o = ctx.enter_context(tc.psum_pool(name="ps_o", bufs=1))
+        ps_t = ctx.enter_context(tc.psum_pool(name="ps_t", bufs=1))
+
+        ident_b = res.tile([P, P], BF16, name="ident_b")
+        make_identity(nc, ident_b[:])
+        ident_f = res.tile([P, P], F32, name="ident_f")
+        make_identity(nc, ident_f[:])
+
+        warm_in = res.tile([P, 1], F32, name="warm_in")
+        warm_out = res.tile([P, 1], F32, name="warm_out")
+        nc.vector.memset(warm_in[:], 0.0)
+        nc.scalar.activation(out=warm_out[:], in_=warm_in[:], func=ACT.Exp)
+
+        q_sb = [res.tile([P, NBLK, C], BF16, name="q_sb%d" % i) for i in range(NWIN)]
+        k_sb = [res.tile([P, NBLK, C], BF16, name="k_sb%d" % i) for i in range(NWIN)]
+        v_sb = [res.tile([P, NBLK, C], BF16, name="v_sb%d" % i) for i in range(NWIN)]
+        q_t = [res.tile([P, NBLK, P], F32, name="q_t%d" % i) for i in range(NWIN)]
+        k_t = [res.tile([P, NBLK, P], F32, name="k_t%d" % i) for i in range(NWIN)]
+        v_codes = [res.tile([P, 2 * C], U32, name="v_codes%d" % i, align_bytes=64) for i in range(NWIN)]
+        v_scales = [res.tile([P, 2 * C], U8, name="v_scales%d" % i, align_bytes=64) for i in range(NWIN)]
+        mask_sb = [res.tile([P, L], BF16, name="mask%d" % i) for i in range(NWIN * NBLK)]
+
+        def load_block(dst, src, win, blk):
+            yq, xo8 = image_block(win, blk)
+            nc.sync.dma_start(out=dst[win][:, blk, :], in_=src[0, yq, xo8])
+
+        def load_mask(win, blk):
+            yh, xo = divmod(blk, 4)
+            nc.sync.dma_start(out=mask_sb[NBLK * win + blk][:], in_=m_blk[win, yh, xo])
+
+        load_block(q_sb, q_blk, 0, 0)
+        for blk in range(4):
+            load_block(k_sb, k_blk, 0, blk)
+        load_mask(0, 0)
+        for blk in range(4, 8):
+            load_block(k_sb, k_blk, 0, blk)
+        for blk in range(1, 8):
+            load_block(q_sb, q_blk, 0, blk)
+        load_mask(0, 1)
+        for blk in range(8):
+            load_block(v_sb, v_blk, 0, blk)
+        for blk in range(2, 8):
+            load_mask(0, blk)
+        for win in range(1, NWIN):
+            for blk in range(8):
+                load_block(k_sb, k_blk, win, blk)
+            for blk in range(8):
+                load_block(q_sb, q_blk, win, blk)
+            for blk in range(8):
+                load_block(v_sb, v_blk, win, blk)
+            for blk in range(8):
+                load_mask(win, blk)
+
+        def flip(dst, src, win, group, on_vector):
+            bank = ps_t.tile([P, 4, P], F32, name="bank", tag="bank")
+            n = len(group)
+            for i, blk in enumerate(group):
+                nc.tensor.transpose(
+                    out=bank[:, i, :], in_=src[win][:, blk, :].bitcast(F32), identity=ident_f[:]
+                )
+            dst_ap = dst[win][:, group[0] : group[0] + n, :]
+            if on_vector:
+                nc.vector.tensor_copy(out=dst_ap, in_=bank[:, 0:n, :])
+            else:
+                nc.scalar.copy(out=dst_ap, in_=bank[:, 0:n, :])
+
+        def scale_q(win, lo, hi):
+            part = q_sb[win][:, lo:hi, :]
+            nc.gpsimd.tensor_scalar(
+                out=part, in0=part, scalar1=0.0625, scalar2=0.0, op0=ALU.mult, op1=ALU.add
+            )
+
+        def prep_v(win):
+            vg = work.tile([P, 2, C, 4], BF16, name="vg", tag="vg", bufs=2, align_bytes=64)
+            nc.gpsimd.tensor_scalar(
+                out=vg[:],
+                in0=v_sb[win][:].rearrange("p (g j) c -> p g c j", g=2, j=4),
+                scalar1=1.0,
+                scalar2=0.0,
+                op0=ALU.mult,
+                op1=ALU.add,
+            )
+            nc.vector.quantize_mx(
+                out=v_codes[win][:].bitcast(FP8X4),
+                scales=v_scales[win][:],
+                in_=vg[:].rearrange("p g c j -> p (g c j)"),
+            )
+
+        def prep_first():
+            scale_q(0, 0, 1)
+            flip(q_t, q_sb, 0, [0], False)
+            flip(k_t, k_sb, 0, [0, 1, 2, 3], True)
+            flip(k_t, k_sb, 0, [4, 5, 6, 7], False)
+
+        def prep_first_rest():
+            scale_q(0, 1, 8)
+            flip(q_t, q_sb, 0, [1, 2, 3], True)
+            flip(q_t, q_sb, 0, [4, 5, 6, 7], False)
+            prep_v(0)
+
+        def prep(win):
+            scale_q(win, 0, 8)
+            flip(k_t, k_sb, win, [0, 1, 2, 3], False)
+            flip(k_t, k_sb, win, [4, 5, 6, 7], False)
+            flip(q_t, q_sb, win, [0, 1, 2, 3], False)
+            flip(q_t, q_sb, win, [4, 5, 6, 7], False)
+            prep_v(win)
+
+        live = {}
+
+        def front(t):
+            win, blk = divmod(t, NBLK)
+            q_pair = q_t[win][:].bitcast(BF16).rearrange("p b (t e) -> p b t e", e=2)
+            k_pair = k_t[win][:].bitcast(BF16).rearrange("p b (t e) -> p b t e", e=2)
+            x = work.tile([P, L], F32, name="x", tag="x")
+            for half in range(2):
+                s_ps = ps_s.tile([P, 512], F32, name="s_ps%d" % half, tag="s_ps%d" % half)
+                for e in range(2):
+                    nc.tensor.matmul(
+                        out=s_ps[:],
+                        lhsT=q_pair[:, blk, :, e],
+                        rhs=k_pair[:, 4 * half : 4 * half + 4, :, e],
+                        start=(e == 0),
+                        stop=(e == 1),
+                    )
+                cols = slice(512 * half, 512 * half + 512)
+                nc.vector.tensor_tensor(
+                    out=x[:, cols].rearrange("p (xo rr xi) -> p xo rr xi", xo=4, rr=16, xi=8),
+                    in0=s_ps[:].rearrange("p (xo rr xi) -> p xo rr xi", xo=4, rr=16, xi=8),
+                    in1=mask_sb[t][:, cols].rearrange("p (rr xo xi) -> p xo rr xi", rr=16, xo=4, xi=8),
+                    op=ALU.add,
+                )
+            neg_max = stat.tile([P, 1], F32, name="neg_max", tag="neg_max")
+            nc.vector.tensor_reduce(out=neg_max[:], in_=x[:], axis=AX.X, op=ALU.max, negate=True)
+            e_sb = work.tile([P, L], BF16, name="e_sb", tag="e_sb")
+            row_sum = stat.tile([P, 1], F32, name="row_sum", tag="row_sum")
+            nc.scalar.activation(
+                out=e_sb[:], in_=x[:], func=ACT.Exp, bias=neg_max[:, 0:1], scale=1.0, accum_out=row_sum[:, 0:1]
+            )
+            live[t] = (e_sb, row_sum)
+
+        def back(t):
+            win, blk = divmod(t, NBLK)
+            e_sb, row_sum = live[t]
+            e_t = ps_e.tile([P, NBLK, P], BF16, name="e_t", tag="e_t")
+            for b in range(NBLK):
+                nc.tensor.transpose(out=e_t[:, b, :], in_=e_sb[:, P * b : P * b + P], identity=ident_b[:])
+            grouped = work.tile([P, 2, P, 4], BF16, name="grouped", tag="grouped", align_bytes=64)
+            nc.scalar.copy(out=grouped[:], in_=e_t[:].rearrange("p (g j) q -> p g q j", g=2, j=4))
+            codes = work.tile([P, 2 * P], U32, name="codes", tag="codes", align_bytes=64)
+            scales = work.tile([P, 2 * P], U8, name="scales", tag="scales", align_bytes=64)
+            nc.vector.quantize_mx(
+                out=codes[:].bitcast(FP8X4),
+                scales=scales[:],
+                in_=grouped[:].rearrange("p g q j -> p (g q j)"),
+            )
+            o_ps = ps_o.tile([P, C], F32, name="o_ps", tag="o_ps")
+            for g in range(2):
+                nc.tensor.matmul_mx(
+                    out=o_ps[:],
+                    lhsT=codes[:, P * g : P * g + P].bitcast(FP8X4),
+                    lhsT_scale=scales[:, P * g : P * g + P],
+                    rhs=v_codes[win][:, C * g : C * g + C].bitcast(FP8X4),
+                    rhs_scale=v_scales[win][:, C * g : C * g + C],
+                    start=(g == 0),
+                    stop=(g == 1),
+                )
+            recip = stat.tile([P, 1], F32, name="recip", tag="recip")
+            nc.vector.reciprocal(out=recip[:], in_=row_sum[:])
+            o_sb = work.tile([P, C], F32, name="o_sb", tag="o_sb", bufs=4)
+            if t % 2 == 1:
+                nc.vector.tensor_scalar(
+                    out=o_sb[:], in0=o_ps[:], scalar1=recip[:, 0:1], scalar2=None, op0=ALU.mult
+                )
+            else:
+                nc.scalar.activation(out=o_sb[:], in_=o_ps[:], func=ACT.Copy, scale=recip[:, 0:1])
+            yq, xo8 = image_block(win, blk)
+            nc.gpsimd.dma_start(out=o_blk[0, yq, xo8], in_=o_sb[:])
+
+        prep_first()
+        for t in range(NWIN * NBLK):
+            win, blk = divmod(t, NBLK)
+            if blk == 2 and win + 1 < NWIN:
+                prep(win + 1)
+            front(t)
+            if t == 0:
+                prep_first_rest()
+            back(t)

@@ -19,6 +19,7 @@ C = 256
 NWIN = 4
 NBLK = 8
 L = 1024
+NT = NWIN * NBLK
 
 
 def image_block(win, blk):
@@ -40,18 +41,19 @@ def tile_single_head_split_window_attention_t_kernel(
     m_blk = attn_mask.rearrange("j (yh rr xo xi) n -> j yh xo rr xi n", yh=2, rr=16, xo=4, xi=8)
 
     with ExitStack() as ctx:
+        ctx.enter_context(tc.manual_schedule())
         res = ctx.enter_context(tc.tile_pool(name="res", bufs=1))
         work = ctx.enter_context(tc.tile_pool(name="work", bufs=3))
-        stat = ctx.enter_context(tc.tile_pool(name="stat", bufs=4))
+        stat = ctx.enter_context(tc.tile_pool(name="stat", bufs=6))
         ps_s = ctx.enter_context(tc.psum_pool(name="ps_s", bufs=2))
         ps_e = ctx.enter_context(tc.psum_pool(name="ps_e", bufs=2))
         ps_o = ctx.enter_context(tc.psum_pool(name="ps_o", bufs=1))
         ps_t = ctx.enter_context(tc.psum_pool(name="ps_t", bufs=1))
 
         ident_b = res.tile([P, P], BF16, name="ident_b")
-        make_identity(nc, ident_b[:])
         ident_f = res.tile([P, P], F32, name="ident_f")
         make_identity(nc, ident_f[:])
+        make_identity(nc, ident_b[:])
 
         warm_in = res.tile([P, 1], F32, name="warm_in")
         warm_out = res.tile([P, 1], F32, name="warm_out")
@@ -65,7 +67,7 @@ def tile_single_head_split_window_attention_t_kernel(
         k_t = [res.tile([P, NBLK, P], F32, name="k_t%d" % i) for i in range(NWIN)]
         v_codes = [res.tile([P, 2 * C], U32, name="v_codes%d" % i, align_bytes=64) for i in range(NWIN)]
         v_scales = [res.tile([P, 2 * C], U8, name="v_scales%d" % i, align_bytes=64) for i in range(NWIN)]
-        mask_sb = [res.tile([P, L], BF16, name="mask%d" % i) for i in range(NWIN * NBLK)]
+        mask_sb = [res.tile([P, L], BF16, name="mask%d" % i) for i in range(NT)]
 
         def load_block(dst, src, win, blk):
             yq, xo8 = image_block(win, blk)
@@ -98,13 +100,16 @@ def tile_single_head_split_window_attention_t_kernel(
             for blk in range(8):
                 load_mask(win, blk)
 
-        def flip(dst, src, win, group, on_vector):
-            bank = ps_t.tile([P, 4, P], F32, name="bank", tag="bank")
-            n = len(group)
+        def flip_pe(src, win, group, pool, tag):
+            bank = pool.tile([P, 4, P], F32, name=tag, tag=tag)
             for i, blk in enumerate(group):
                 nc.tensor.transpose(
                     out=bank[:, i, :], in_=src[win][:, blk, :].bitcast(F32), identity=ident_f[:]
                 )
+            return bank
+
+        def flip_out(dst, win, group, bank, on_vector):
+            n = len(group)
             dst_ap = dst[win][:, group[0] : group[0] + n, :]
             if on_vector:
                 nc.vector.tensor_copy(out=dst_ap, in_=bank[:, 0:n, :])
@@ -117,7 +122,9 @@ def tile_single_head_split_window_attention_t_kernel(
                 out=part, in0=part, scalar1=0.0625, scalar2=0.0, op0=ALU.mult, op1=ALU.add
             )
 
-        def prep_v(win):
+        v_grouped = {}
+
+        def group_v(win):
             vg = work.tile([P, 2, C, 4], BF16, name="vg", tag="vg", bufs=2, align_bytes=64)
             nc.gpsimd.tensor_scalar(
                 out=vg[:],
@@ -127,84 +134,99 @@ def tile_single_head_split_window_attention_t_kernel(
                 op0=ALU.mult,
                 op1=ALU.add,
             )
+            v_grouped[win] = vg
+
+        def quantise_v(win):
             nc.vector.quantize_mx(
                 out=v_codes[win][:].bitcast(FP8X4),
                 scales=v_scales[win][:],
-                in_=vg[:].rearrange("p g c j -> p (g c j)"),
+                in_=v_grouped[win][:].rearrange("p g c j -> p (g c j)"),
             )
 
-        def prep_first():
-            scale_q(0, 0, 1)
-            flip(q_t, q_sb, 0, [0], False)
-            flip(k_t, k_sb, 0, [0, 1, 2, 3], True)
-            flip(k_t, k_sb, 0, [4, 5, 6, 7], False)
+        s_tiles = {}
+        x_tiles = {}
+        e_tiles = {}
+        et_tiles = {}
+        g_tiles = {}
+        c_tiles = {}
+        o_tiles = {}
+        sums = {}
+        negs = {}
+        recips = {}
 
-        def prep_first_rest():
-            scale_q(0, 1, 8)
-            flip(q_t, q_sb, 0, [1, 2, 3], True)
-            flip(q_t, q_sb, 0, [4, 5, 6, 7], False)
-            prep_v(0)
-
-        def prep(win):
-            scale_q(win, 0, 8)
-            flip(k_t, k_sb, win, [0, 1, 2, 3], False)
-            flip(k_t, k_sb, win, [4, 5, 6, 7], False)
-            flip(q_t, q_sb, win, [0, 1, 2, 3], False)
-            flip(q_t, q_sb, win, [4, 5, 6, 7], False)
-            prep_v(win)
-
-        live = {}
-
-        def front(t):
+        def score_mm(t, half, e):
             win, blk = divmod(t, NBLK)
             q_pair = q_t[win][:].bitcast(BF16).rearrange("p b (t e) -> p b t e", e=2)
             k_pair = k_t[win][:].bitcast(BF16).rearrange("p b (t e) -> p b t e", e=2)
+            if e == 0:
+                s_tiles[(t, half)] = ps_s.tile([P, 512], F32, name="s_ps%d" % half, tag="s_ps%d" % half)
+            nc.tensor.matmul(
+                out=s_tiles[(t, half)][:],
+                lhsT=q_pair[:, blk, :, e],
+                rhs=k_pair[:, 4 * half : 4 * half + 4, :, e],
+                start=(e == 0),
+                stop=(e == 1),
+            )
+
+        def flip_e(t, lo, hi):
+            if lo == 0:
+                et_tiles[t] = ps_e.tile([P, NBLK, P], BF16, name="e_t", tag="e_t")
+            for b in range(lo, hi):
+                nc.tensor.transpose(
+                    out=et_tiles[t][:, b, :], in_=e_tiles[t][:, P * b : P * b + P], identity=ident_b[:]
+                )
+
+        def add_mask_and_max(t):
             x = work.tile([P, L], F32, name="x", tag="x")
+            x_tiles[t] = x
             for half in range(2):
-                s_ps = ps_s.tile([P, 512], F32, name="s_ps%d" % half, tag="s_ps%d" % half)
-                for e in range(2):
-                    nc.tensor.matmul(
-                        out=s_ps[:],
-                        lhsT=q_pair[:, blk, :, e],
-                        rhs=k_pair[:, 4 * half : 4 * half + 4, :, e],
-                        start=(e == 0),
-                        stop=(e == 1),
-                    )
                 cols = slice(512 * half, 512 * half + 512)
                 nc.vector.tensor_tensor(
                     out=x[:, cols].rearrange("p (xo rr xi) -> p xo rr xi", xo=4, rr=16, xi=8),
-                    in0=s_ps[:].rearrange("p (xo rr xi) -> p xo rr xi", xo=4, rr=16, xi=8),
+                    in0=s_tiles[(t, half)][:].rearrange("p (xo rr xi) -> p xo rr xi", xo=4, rr=16, xi=8),
                     in1=mask_sb[t][:, cols].rearrange("p (rr xo xi) -> p xo rr xi", rr=16, xo=4, xi=8),
                     op=ALU.add,
                 )
-            neg_max = stat.tile([P, 1], F32, name="neg_max", tag="neg_max")
-            nc.vector.tensor_reduce(out=neg_max[:], in_=x[:], axis=AX.X, op=ALU.max, negate=True)
-            e_sb = work.tile([P, L], BF16, name="e_sb", tag="e_sb")
-            row_sum = stat.tile([P, 1], F32, name="row_sum", tag="row_sum")
-            nc.scalar.activation(
-                out=e_sb[:], in_=x[:], func=ACT.Exp, bias=neg_max[:, 0:1], scale=1.0, accum_out=row_sum[:, 0:1]
-            )
-            live[t] = (e_sb, row_sum)
+            negs[t] = stat.tile([P, 1], F32, name="neg_max", tag="neg_max")
+            nc.vector.tensor_reduce(out=negs[t][:], in_=x[:], axis=AX.X, op=ALU.max, negate=True)
 
-        def back(t):
-            win, blk = divmod(t, NBLK)
-            e_sb, row_sum = live[t]
-            e_t = ps_e.tile([P, NBLK, P], BF16, name="e_t", tag="e_t")
-            for b in range(NBLK):
-                nc.tensor.transpose(out=e_t[:, b, :], in_=e_sb[:, P * b : P * b + P], identity=ident_b[:])
-            grouped = work.tile([P, 2, P, 4], BF16, name="grouped", tag="grouped", align_bytes=64)
-            nc.scalar.copy(out=grouped[:], in_=e_t[:].rearrange("p (g j) q -> p g q j", g=2, j=4))
+        def exponent(t):
+            e_tiles[t] = work.tile([P, L], BF16, name="e_sb", tag="e_sb")
+            sums[t] = stat.tile([P, 1], F32, name="row_sum", tag="row_sum")
+            nc.scalar.activation(
+                out=e_tiles[t][:],
+                in_=x_tiles[t][:],
+                func=ACT.Exp,
+                bias=negs[t][:, 0:1],
+                scale=1.0,
+                accum_out=sums[t][:, 0:1],
+            )
+
+        def reciprocal(t):
+            recips[t] = stat.tile([P, 1], F32, name="recip", tag="recip")
+            nc.vector.reciprocal(out=recips[t][:], in_=sums[t][:])
+
+        def regroup(t):
+            g_tiles[t] = work.tile([P, 2, P, 4], BF16, name="grouped", tag="grouped", align_bytes=64)
+            nc.scalar.copy(out=g_tiles[t][:], in_=et_tiles[t][:].rearrange("p (g j) q -> p g q j", g=2, j=4))
+
+        def quantise_e(t):
             codes = work.tile([P, 2 * P], U32, name="codes", tag="codes", align_bytes=64)
             scales = work.tile([P, 2 * P], U8, name="scales", tag="scales", align_bytes=64)
+            c_tiles[t] = (codes, scales)
             nc.vector.quantize_mx(
                 out=codes[:].bitcast(FP8X4),
                 scales=scales[:],
-                in_=grouped[:].rearrange("p g q j -> p (g q j)"),
+                in_=g_tiles[t][:].rearrange("p g q j -> p (g q j)"),
             )
-            o_ps = ps_o.tile([P, C], F32, name="o_ps", tag="o_ps")
+
+        def weighted_sum(t):
+            win = t // NBLK
+            codes, scales = c_tiles[t]
+            o_tiles[t] = ps_o.tile([P, C], F32, name="o_ps", tag="o_ps")
             for g in range(2):
                 nc.tensor.matmul_mx(
-                    out=o_ps[:],
+                    out=o_tiles[t][:],
                     lhsT=codes[:, P * g : P * g + P].bitcast(FP8X4),
                     lhsT_scale=scales[:, P * g : P * g + P],
                     rhs=v_codes[win][:, C * g : C * g + C].bitcast(FP8X4),
@@ -212,24 +234,87 @@ def tile_single_head_split_window_attention_t_kernel(
                     start=(g == 0),
                     stop=(g == 1),
                 )
-            recip = stat.tile([P, 1], F32, name="recip", tag="recip")
-            nc.vector.reciprocal(out=recip[:], in_=row_sum[:])
+
+        def finish(t, on_vector):
+            win, blk = divmod(t, NBLK)
             o_sb = work.tile([P, C], F32, name="o_sb", tag="o_sb", bufs=4)
-            if t % 2 == 1:
+            if on_vector:
                 nc.vector.tensor_scalar(
-                    out=o_sb[:], in0=o_ps[:], scalar1=recip[:, 0:1], scalar2=None, op0=ALU.mult
+                    out=o_sb[:], in0=o_tiles[t][:], scalar1=recips[t][:, 0:1], scalar2=None, op0=ALU.mult
                 )
             else:
-                nc.scalar.activation(out=o_sb[:], in_=o_ps[:], func=ACT.Copy, scale=recip[:, 0:1])
+                nc.scalar.activation(out=o_sb[:], in_=o_tiles[t][:], func=ACT.Copy, scale=recips[t][:, 0:1])
             yq, xo8 = image_block(win, blk)
             nc.gpsimd.dma_start(out=o_blk[0, yq, xo8], in_=o_sb[:])
 
-        prep_first()
-        for t in range(NWIN * NBLK):
-            win, blk = divmod(t, NBLK)
-            if blk == 2 and win + 1 < NWIN:
-                prep(win + 1)
-            front(t)
-            if t == 0:
-                prep_first_rest()
-            back(t)
+        def finish_on_vector(t):
+            return t % NBLK in (1, 2, 3, 4)
+
+        def valid(t):
+            return 0 <= t < NT
+
+        scale_q(0, 0, 1)
+        bank = flip_pe(k_sb, 0, [0, 1, 2, 3], ps_s, "s_ps0")
+        flip_out(k_t, 0, [0, 1, 2, 3], bank, True)
+        bank = flip_pe(q_sb, 0, [0], ps_s, "s_ps1")
+        flip_out(q_t, 0, [0], bank, False)
+        bank = flip_pe(k_sb, 0, [4, 5, 6, 7], ps_s, "s_ps0")
+        flip_out(k_t, 0, [4, 5, 6, 7], bank, False)
+        for half in range(2):
+            for e in range(2):
+                score_mm(0, half, e)
+        scale_q(0, 1, 4)
+        scale_q(0, 4, 8)
+        group_v(0)
+        bank = flip_pe(q_sb, 0, [1, 2, 3], ps_s, "s_ps1")
+        flip_out(q_t, 0, [1, 2, 3], bank, False)
+        bank = flip_pe(q_sb, 0, [4, 5, 6, 7], ps_s, "s_ps0")
+        flip_out(q_t, 0, [4, 5, 6, 7], bank, False)
+
+        flips = {3: (k_sb, k_t, [0, 1, 2, 3]), 4: (k_sb, k_t, [4, 5, 6, 7]), 5: (q_sb, q_t, [0, 1, 2, 3]), 6: (q_sb, q_t, [4, 5, 6, 7])}
+
+        for tau in range(NT + 3):
+            win, blk = divmod(tau, NBLK)
+            nxt = win + 1
+            prep = nxt < NWIN
+            if prep and blk == 2:
+                scale_q(nxt, 0, 8)
+                group_v(nxt)
+            if valid(tau + 1):
+                score_mm(tau + 1, 0, 0)
+            if valid(tau - 1):
+                flip_e(tau - 1, 0, 3)
+            if valid(tau + 1):
+                score_mm(tau + 1, 0, 1)
+            if valid(tau - 1):
+                flip_e(tau - 1, 3, 6)
+            if valid(tau + 1):
+                score_mm(tau + 1, 1, 0)
+            if valid(tau - 1):
+                flip_e(tau - 1, 6, 8)
+            bank = None
+            if prep and blk in flips:
+                bank = flip_pe(flips[blk][0], nxt, flips[blk][2], ps_t, "bank")
+            if valid(tau + 1):
+                score_mm(tau + 1, 1, 1)
+            if valid(tau):
+                add_mask_and_max(tau)
+            if valid(tau - 1):
+                reciprocal(tau - 1)
+            if valid(tau):
+                exponent(tau)
+            if valid(tau - 1):
+                regroup(tau - 1)
+            if bank is not None:
+                flip_out(flips[blk][1], nxt, flips[blk][2], bank, False)
+            if valid(tau - 3) and finish_on_vector(tau - 3):
+                finish(tau - 3, True)
+            if tau == 1:
+                quantise_v(0)
+            if prep and blk == 6:
+                quantise_v(nxt)
+            if valid(tau - 2):
+                quantise_e(tau - 2)
+                weighted_sum(tau - 2)
+                if not finish_on_vector(tau - 2):
+                    finish(tau - 2, False)

@@ -20,6 +20,7 @@ NWIN = 4
 NBLK = 8
 L = 1024
 NT = NWIN * NBLK
+SYNC_STORES_FROM = 16
 
 
 def image_block(win, blk):
@@ -176,7 +177,7 @@ def tile_single_head_split_window_attention_t_kernel(
                     out=et_tiles[t][:, b, :], in_=e_tiles[t][:, P * b : P * b + P], identity=ident_b[:]
                 )
 
-        def add_mask_and_max(t):
+        def add_mask(t):
             x = work.tile([P, L], F32, name="x", tag="x")
             x_tiles[t] = x
             for half in range(2):
@@ -187,8 +188,10 @@ def tile_single_head_split_window_attention_t_kernel(
                     in1=mask_sb[t][:, cols].rearrange("p (rr xo xi) -> p xo rr xi", rr=16, xo=4, xi=8),
                     op=ALU.add,
                 )
+
+        def row_max(t):
             negs[t] = stat.tile([P, 1], F32, name="neg_max", tag="neg_max")
-            nc.vector.tensor_reduce(out=negs[t][:], in_=x[:], axis=AX.X, op=ALU.max, negate=True)
+            nc.vector.tensor_reduce(out=negs[t][:], in_=x_tiles[t][:], axis=AX.X, op=ALU.max, negate=True)
 
         def exponent(t):
             e_tiles[t] = work.tile([P, L], BF16, name="e_sb", tag="e_sb")
@@ -208,7 +211,11 @@ def tile_single_head_split_window_attention_t_kernel(
 
         def regroup(t):
             g_tiles[t] = work.tile([P, 2, P, 4], BF16, name="grouped", tag="grouped", align_bytes=64)
-            nc.scalar.copy(out=g_tiles[t][:], in_=et_tiles[t][:].rearrange("p (g j) q -> p g q j", g=2, j=4))
+            src = et_tiles[t][:].rearrange("p (g j) q -> p g q j", g=2, j=4)
+            if t == NT - 2:
+                nc.vector.tensor_copy(out=g_tiles[t][:], in_=src)
+            else:
+                nc.scalar.copy(out=g_tiles[t][:], in_=src)
 
         def quantise_e(t):
             codes = work.tile([P, 2 * P], U32, name="codes", tag="codes", align_bytes=64)
@@ -245,10 +252,13 @@ def tile_single_head_split_window_attention_t_kernel(
             else:
                 nc.scalar.activation(out=o_sb[:], in_=o_tiles[t][:], func=ACT.Copy, scale=recips[t][:, 0:1])
             yq, xo8 = image_block(win, blk)
-            nc.gpsimd.dma_start(out=o_blk[0, yq, xo8], in_=o_sb[:])
+            if t < SYNC_STORES_FROM:
+                nc.gpsimd.dma_start(out=o_blk[0, yq, xo8], in_=o_sb[:])
+            else:
+                nc.sync.dma_start(out=o_blk[0, yq, xo8], in_=o_sb[:])
 
         def finish_on_vector(t):
-            return t % NBLK in (1, 2, 3, 4)
+            return t % NBLK in (0, 1, 2, 3) or t >= NT - 4
 
         def valid(t):
             return 0 <= t < NT
@@ -273,7 +283,7 @@ def tile_single_head_split_window_attention_t_kernel(
 
         flips = {3: (k_sb, k_t, [0, 1, 2, 3]), 4: (k_sb, k_t, [4, 5, 6, 7]), 5: (q_sb, q_t, [0, 1, 2, 3]), 6: (q_sb, q_t, [4, 5, 6, 7])}
 
-        for tau in range(NT + 3):
+        for tau in range(NT + 4):
             win, blk = divmod(tau, NBLK)
             nxt = win + 1
             prep = nxt < NWIN
@@ -282,39 +292,37 @@ def tile_single_head_split_window_attention_t_kernel(
                 group_v(nxt)
             if valid(tau + 1):
                 score_mm(tau + 1, 0, 0)
-            if valid(tau - 1):
-                flip_e(tau - 1, 0, 3)
-            if valid(tau + 1):
                 score_mm(tau + 1, 0, 1)
             if valid(tau - 1):
-                flip_e(tau - 1, 3, 6)
+                exponent(tau - 1)
+                flip_e(tau - 1, 0, 3)
             if valid(tau + 1):
                 score_mm(tau + 1, 1, 0)
+            if valid(tau):
+                add_mask(tau)
+            if valid(tau - 4) and finish_on_vector(tau - 4):
+                finish(tau - 4, True)
+            if valid(tau - 3):
+                quantise_e(tau - 3)
+                weighted_sum(tau - 3)
+            if valid(tau + 1):
+                score_mm(tau + 1, 1, 1)
             if valid(tau - 1):
-                flip_e(tau - 1, 6, 8)
+                flip_e(tau - 1, 3, 8)
             bank = None
             if prep and blk in flips:
                 bank = flip_pe(flips[blk][0], nxt, flips[blk][2], ps_t, "bank")
-            if valid(tau + 1):
-                score_mm(tau + 1, 1, 1)
-            if valid(tau):
-                add_mask_and_max(tau)
-            if valid(tau - 1):
-                reciprocal(tau - 1)
-            if valid(tau):
-                exponent(tau)
-            if valid(tau - 1):
-                regroup(tau - 1)
-            if bank is not None:
-                flip_out(flips[blk][1], nxt, flips[blk][2], bank, False)
-            if valid(tau - 3) and finish_on_vector(tau - 3):
-                finish(tau - 3, True)
+            if valid(tau - 2):
+                reciprocal(tau - 2)
             if tau == 1:
                 quantise_v(0)
             if prep and blk == 6:
                 quantise_v(nxt)
+            if valid(tau):
+                row_max(tau)
             if valid(tau - 2):
-                quantise_e(tau - 2)
-                weighted_sum(tau - 2)
-                if not finish_on_vector(tau - 2):
-                    finish(tau - 2, False)
+                regroup(tau - 2)
+            if bank is not None:
+                flip_out(flips[blk][1], nxt, flips[blk][2], bank, False)
+            if valid(tau - 3) and not finish_on_vector(tau - 3):
+                finish(tau - 3, False)

@@ -45,11 +45,10 @@ def tile_single_head_split_window_attention_t_kernel(
         ctx.enter_context(tc.manual_schedule())
         res = ctx.enter_context(tc.tile_pool(name="res", bufs=1))
         work = ctx.enter_context(tc.tile_pool(name="work", bufs=3))
-        stat = ctx.enter_context(tc.tile_pool(name="stat", bufs=6))
+        stat = ctx.enter_context(tc.tile_pool(name="stat", bufs=8))
         ps_s = ctx.enter_context(tc.psum_pool(name="ps_s", bufs=2))
         ps_e = ctx.enter_context(tc.psum_pool(name="ps_e", bufs=2))
-        ps_o = ctx.enter_context(tc.psum_pool(name="ps_o", bufs=1))
-        ps_t = ctx.enter_context(tc.psum_pool(name="ps_t", bufs=1))
+        ps_m = ctx.enter_context(tc.psum_pool(name="ps_m", bufs=2))
 
         ident_b = res.tile([P, P], BF16, name="ident_b")
         ident_f = res.tile([P, P], F32, name="ident_f")
@@ -102,7 +101,7 @@ def tile_single_head_split_window_attention_t_kernel(
                 load_mask(win, blk)
 
         def flip_pe(src, win, group, pool, tag):
-            bank = pool.tile([P, 4, P], F32, name=tag, tag=tag)
+            bank = pool.tile([P, 4, P], F32, name="bank_" + tag, tag=tag)
             for i, blk in enumerate(group):
                 nc.tensor.transpose(
                     out=bank[:, i, :], in_=src[win][:, blk, :].bitcast(F32), identity=ident_f[:]
@@ -127,14 +126,17 @@ def tile_single_head_split_window_attention_t_kernel(
 
         def group_v(win):
             vg = work.tile([P, 2, C, 4], BF16, name="vg", tag="vg", bufs=2, align_bytes=64)
-            nc.gpsimd.tensor_scalar(
-                out=vg[:],
-                in0=v_sb[win][:].rearrange("p (g j) c -> p g c j", g=2, j=4),
-                scalar1=1.0,
-                scalar2=0.0,
-                op0=ALU.mult,
-                op1=ALU.add,
-            )
+            src = v_sb[win][:].rearrange("p (g j) c -> p g c j", g=2, j=4)
+            for g in range(2):
+                for lo in range(0, C, P):
+                    nc.gpsimd.tensor_scalar(
+                        out=vg[:, g, lo : lo + P, :],
+                        in0=src[:, g, lo : lo + P, :],
+                        scalar1=1.0,
+                        scalar2=0.0,
+                        op0=ALU.mult,
+                        op1=ALU.add,
+                    )
             v_grouped[win] = vg
 
         def quantise_v(win):
@@ -212,7 +214,7 @@ def tile_single_head_split_window_attention_t_kernel(
         def regroup(t):
             g_tiles[t] = work.tile([P, 2, P, 4], BF16, name="grouped", tag="grouped", align_bytes=64)
             src = et_tiles[t][:].rearrange("p (g j) q -> p g q j", g=2, j=4)
-            if t == NT - 2:
+            if t in (NT - 3, NT - 2):
                 nc.vector.tensor_copy(out=g_tiles[t][:], in_=src)
             else:
                 nc.scalar.copy(out=g_tiles[t][:], in_=src)
@@ -230,7 +232,7 @@ def tile_single_head_split_window_attention_t_kernel(
         def weighted_sum(t):
             win = t // NBLK
             codes, scales = c_tiles[t]
-            o_tiles[t] = ps_o.tile([P, C], F32, name="o_ps", tag="o_ps")
+            o_tiles[t] = ps_m.tile([P, C], F32, name="o_ps", tag="misc")
             for g in range(2):
                 nc.tensor.matmul_mx(
                     out=o_tiles[t][:],
@@ -258,7 +260,7 @@ def tile_single_head_split_window_attention_t_kernel(
                 nc.sync.dma_start(out=o_blk[0, yq, xo8], in_=o_sb[:])
 
         def finish_on_vector(t):
-            return t % NBLK in (0, 1, 2, 3) or t >= NT - 4
+            return t % NBLK in (6, 7, 0, 1) or t >= NT - 5
 
         def valid(t):
             return 0 <= t < NT
@@ -283,35 +285,32 @@ def tile_single_head_split_window_attention_t_kernel(
 
         flips = {3: (k_sb, k_t, [0, 1, 2, 3]), 4: (k_sb, k_t, [4, 5, 6, 7]), 5: (q_sb, q_t, [0, 1, 2, 3]), 6: (q_sb, q_t, [4, 5, 6, 7])}
 
-        for tau in range(NT + 4):
+        for tau in range(NT + 5):
             win, blk = divmod(tau, NBLK)
             nxt = win + 1
             prep = nxt < NWIN
             if prep and blk == 2:
-                scale_q(nxt, 0, 8)
+                for lo in range(0, NBLK, 2):
+                    scale_q(nxt, lo, lo + 2)
                 group_v(nxt)
             if valid(tau + 1):
-                score_mm(tau + 1, 0, 0)
-                score_mm(tau + 1, 0, 1)
+                for half in range(2):
+                    for e in range(2):
+                        score_mm(tau + 1, half, e)
             if valid(tau - 1):
                 exponent(tau - 1)
-                flip_e(tau - 1, 0, 3)
-            if valid(tau + 1):
-                score_mm(tau + 1, 1, 0)
-            if valid(tau):
-                add_mask(tau)
-            if valid(tau - 4) and finish_on_vector(tau - 4):
-                finish(tau - 4, True)
-            if valid(tau - 3):
-                quantise_e(tau - 3)
-                weighted_sum(tau - 3)
-            if valid(tau + 1):
-                score_mm(tau + 1, 1, 1)
-            if valid(tau - 1):
-                flip_e(tau - 1, 3, 8)
+            if valid(tau - 2):
+                flip_e(tau - 2, 0, 8)
             bank = None
             if prep and blk in flips:
-                bank = flip_pe(flips[blk][0], nxt, flips[blk][2], ps_t, "bank")
+                bank = flip_pe(flips[blk][0], nxt, flips[blk][2], ps_m, "misc")
+            if valid(tau):
+                add_mask(tau)
+            if valid(tau - 5) and finish_on_vector(tau - 5):
+                finish(tau - 5, True)
+            if valid(tau - 4):
+                quantise_e(tau - 4)
+                weighted_sum(tau - 4)
             if valid(tau - 2):
                 reciprocal(tau - 2)
             if tau == 1:
@@ -320,9 +319,9 @@ def tile_single_head_split_window_attention_t_kernel(
                 quantise_v(nxt)
             if valid(tau):
                 row_max(tau)
-            if valid(tau - 2):
-                regroup(tau - 2)
+            if valid(tau - 3):
+                regroup(tau - 3)
             if bank is not None:
                 flip_out(flips[blk][1], nxt, flips[blk][2], bank, False)
-            if valid(tau - 3) and not finish_on_vector(tau - 3):
-                finish(tau - 3, False)
+            if valid(tau - 5) and not finish_on_vector(tau - 5):
+                finish(tau - 5, False)

@@ -19,8 +19,13 @@ C = 256
 NWIN = 4
 NBLK = 8
 L = 1024
+HALF = 512
 NT = NWIN * NBLK
-SYNC_STORES_FROM = 16
+MASK_ON_TENSOR = tuple(range(2, NT, 5))
+FIRST_ROUND_MASK = 3
+ROUNDS_AHEAD = 4
+LAST_VIA_GPSIMD = NT - 3
+INV_SCALE = 0.0625
 
 
 def image_block(win, blk):
@@ -50,10 +55,14 @@ def tile_single_head_split_window_attention_t_kernel(
         ps_e = ctx.enter_context(tc.psum_pool(name="ps_e", bufs=2))
         ps_m = ctx.enter_context(tc.psum_pool(name="ps_m", bufs=2))
 
-        ident_b = res.tile([P, P], BF16, name="ident_b")
         ident_f = res.tile([P, P], F32, name="ident_f")
+        ident_b = res.tile([P, P], BF16, name="ident_b")
+        ident_16 = res.tile([P, P], BF16, name="ident_16")
         make_identity(nc, ident_f[:])
         make_identity(nc, ident_b[:])
+        nc.gpsimd.tensor_scalar(
+            out=ident_16[:], in0=ident_b[:], scalar1=1.0 / INV_SCALE, scalar2=0.0, op0=ALU.mult, op1=ALU.add
+        )
 
         warm_in = res.tile([P, 1], F32, name="warm_in")
         warm_out = res.tile([P, 1], F32, name="warm_out")
@@ -64,41 +73,47 @@ def tile_single_head_split_window_attention_t_kernel(
         k_sb = [res.tile([P, NBLK, C], BF16, name="k_sb%d" % i) for i in range(NWIN)]
         v_sb = [res.tile([P, NBLK, C], BF16, name="v_sb%d" % i) for i in range(NWIN)]
         q_t = [res.tile([P, NBLK, P], F32, name="q_t%d" % i) for i in range(NWIN)]
-        k_t = [res.tile([P, NBLK, P], F32, name="k_t%d" % i) for i in range(NWIN)]
+        k_t = [res.tile([P, 2, HALF], F32, name="k_t%d" % i) for i in range(NWIN)]
         v_codes = [res.tile([P, 2 * C], U32, name="v_codes%d" % i, align_bytes=64) for i in range(NWIN)]
         v_scales = [res.tile([P, 2 * C], U8, name="v_scales%d" % i, align_bytes=64) for i in range(NWIN)]
         mask_sb = [res.tile([P, L], BF16, name="mask%d" % i) for i in range(NT)]
 
-        def load_block(dst, src, win, blk):
-            yq, xo8 = image_block(win, blk)
-            nc.sync.dma_start(out=dst[win][:, blk, :], in_=src[0, yq, xo8])
+        def load_blocks(dst, src, win, lo, hi):
+            for blk in range(lo, hi):
+                yq, xo8 = image_block(win, blk)
+                nc.sync.dma_start(out=dst[win][:, blk, :], in_=src[0, yq, xo8])
 
-        def load_mask(win, blk):
-            yh, xo = divmod(blk, 4)
-            nc.sync.dma_start(out=mask_sb[NBLK * win + blk][:], in_=m_blk[win, yh, xo])
+        def load_masks(lo, hi):
+            for t in range(lo, hi):
+                win, blk = divmod(t, NBLK)
+                yh, xo = divmod(blk, 4)
+                nc.sync.dma_start(out=mask_sb[t][:], in_=m_blk[win, yh, xo])
 
-        load_block(q_sb, q_blk, 0, 0)
-        for blk in range(4):
-            load_block(k_sb, k_blk, 0, blk)
-        load_mask(0, 0)
-        for blk in range(4, 8):
-            load_block(k_sb, k_blk, 0, blk)
-        for blk in range(1, 8):
-            load_block(q_sb, q_blk, 0, blk)
-        load_mask(0, 1)
-        for blk in range(8):
-            load_block(v_sb, v_blk, 0, blk)
-        for blk in range(2, 8):
-            load_mask(0, blk)
+        load_blocks(q_sb, q_blk, 0, 0, 1)
+        load_blocks(k_sb, k_blk, 0, 0, 4)
+        load_masks(0, 1)
+        load_blocks(k_sb, k_blk, 0, 4, 8)
+        load_blocks(q_sb, q_blk, 0, 1, 4)
+        load_masks(1, 2)
+        load_blocks(q_sb, q_blk, 0, 4, 8)
+        load_masks(2, 3)
+        load_blocks(v_sb, v_blk, 0, 0, 8)
+
+        later = []
         for win in range(1, NWIN):
-            for blk in range(8):
-                load_block(k_sb, k_blk, win, blk)
-            for blk in range(8):
-                load_block(q_sb, q_blk, win, blk)
-            for blk in range(8):
-                load_block(v_sb, v_blk, win, blk)
-            for blk in range(8):
-                load_mask(win, blk)
+            for dst, src in ((k_sb, k_blk), (q_sb, q_blk), (v_sb, v_blk)):
+                for lo in range(0, NBLK, 4):
+                    later.append((dst, src, win, lo))
+
+        def load_round(i):
+            if FIRST_ROUND_MASK + i < NT:
+                load_masks(FIRST_ROUND_MASK + i, FIRST_ROUND_MASK + i + 1)
+            if i < len(later):
+                dst, src, win, lo = later[i]
+                load_blocks(dst, src, win, lo, lo + 4)
+
+        for i in range(ROUNDS_AHEAD):
+            load_round(i)
 
         def flip_pe(src, win, group, pool, tag):
             bank = pool.tile([P, 4, P], F32, name="bank_" + tag, tag=tag)
@@ -108,36 +123,37 @@ def tile_single_head_split_window_attention_t_kernel(
                 )
             return bank
 
-        def flip_out(dst, win, group, bank, on_vector):
+        def flip_out_q(win, group, bank, on_vector):
             n = len(group)
-            dst_ap = dst[win][:, group[0] : group[0] + n, :]
+            dst_ap = q_t[win][:, group[0] : group[0] + n, :]
             if on_vector:
                 nc.vector.tensor_copy(out=dst_ap, in_=bank[:, 0:n, :])
             else:
                 nc.scalar.copy(out=dst_ap, in_=bank[:, 0:n, :])
 
-        def scale_q(win, lo, hi):
-            part = q_sb[win][:, lo:hi, :]
-            nc.gpsimd.tensor_scalar(
-                out=part, in0=part, scalar1=0.0625, scalar2=0.0, op0=ALU.mult, op1=ALU.add
-            )
+        def flip_out_k(win, yh, bank, on_vector):
+            dst_ap = k_t[win][:, yh, :].rearrange("p (rr xo xi) -> p rr xo xi", rr=16, xo=4, xi=8)
+            src_ap = bank[:].rearrange("p xo (rr xi) -> p rr xo xi", rr=16, xi=8)
+            if on_vector:
+                nc.vector.tensor_copy(out=dst_ap, in_=src_ap)
+            else:
+                nc.scalar.copy(out=dst_ap, in_=src_ap)
 
         v_grouped = {}
 
-        def group_v(win):
-            vg = work.tile([P, 2, C, 4], BF16, name="vg", tag="vg", bufs=2, align_bytes=64)
+        def group_v(win, piece):
+            if piece == 0:
+                v_grouped[win] = work.tile([P, 2, C, 4], BF16, name="vg", tag="vg", bufs=2, align_bytes=64)
+            g, lo = divmod(piece, 2)
             src = v_sb[win][:].rearrange("p (g j) c -> p g c j", g=2, j=4)
-            for g in range(2):
-                for lo in range(0, C, P):
-                    nc.gpsimd.tensor_scalar(
-                        out=vg[:, g, lo : lo + P, :],
-                        in0=src[:, g, lo : lo + P, :],
-                        scalar1=1.0,
-                        scalar2=0.0,
-                        op0=ALU.mult,
-                        op1=ALU.add,
-                    )
-            v_grouped[win] = vg
+            nc.gpsimd.tensor_scalar(
+                out=v_grouped[win][:, g, P * lo : P * lo + P, :],
+                in0=src[:, g, P * lo : P * lo + P, :],
+                scalar1=1.0,
+                scalar2=0.0,
+                op0=ALU.mult,
+                op1=ALU.add,
+            )
 
         def quantise_v(win):
             nc.vector.quantize_mx(
@@ -147,77 +163,140 @@ def tile_single_head_split_window_attention_t_kernel(
             )
 
         s_tiles = {}
+        halves = {}
         x_tiles = {}
         e_tiles = {}
         et_tiles = {}
         g_tiles = {}
+        lin_tiles = {}
         c_tiles = {}
         o_tiles = {}
         sums = {}
         negs = {}
         recips = {}
 
-        def score_mm(t, half, e):
+        def scores(t):
             win, blk = divmod(t, NBLK)
             q_pair = q_t[win][:].bitcast(BF16).rearrange("p b (t e) -> p b t e", e=2)
-            k_pair = k_t[win][:].bitcast(BF16).rearrange("p b (t e) -> p b t e", e=2)
-            if e == 0:
-                s_tiles[(t, half)] = ps_s.tile([P, 512], F32, name="s_ps%d" % half, tag="s_ps%d" % half)
-            nc.tensor.matmul(
-                out=s_tiles[(t, half)][:],
-                lhsT=q_pair[:, blk, :, e],
-                rhs=k_pair[:, 4 * half : 4 * half + 4, :, e],
-                start=(e == 0),
-                stop=(e == 1),
-            )
-
-        def flip_e(t, lo, hi):
-            if lo == 0:
-                et_tiles[t] = ps_e.tile([P, NBLK, P], BF16, name="e_t", tag="e_t")
-            for b in range(lo, hi):
-                nc.tensor.transpose(
-                    out=et_tiles[t][:, b, :], in_=e_tiles[t][:, P * b : P * b + P], identity=ident_b[:]
-                )
+            k_pair = k_t[win][:].bitcast(BF16).rearrange("p y (t e) -> p y t e", e=2)
+            for half in range(2):
+                s_ps = ps_s.tile([P, HALF], F32, name="s_ps%d" % half, tag="s_ps%d" % half)
+                s_tiles[(t, half)] = s_ps
+                for e in range(2):
+                    nc.tensor.matmul(
+                        out=s_ps[:],
+                        lhsT=q_pair[:, blk, :, e],
+                        rhs=k_pair[:, half, :, e],
+                        start=(e == 0),
+                        stop=(e == 1 and t not in MASK_ON_TENSOR),
+                    )
+                if t in MASK_ON_TENSOR:
+                    nc.tensor.matmul(
+                        out=s_ps[:],
+                        lhsT=ident_16[:],
+                        rhs=mask_sb[t][:, HALF * half : HALF * half + HALF],
+                        start=False,
+                        stop=True,
+                    )
 
         def add_mask(t):
+            if t in MASK_ON_TENSOR:
+                halves[t] = stat.tile([P, 2], F32, name="half_max", tag="half_max")
+                for half in range(2):
+                    nc.vector.tensor_reduce(
+                        out=halves[t][:, half : half + 1], in_=s_tiles[(t, half)][:], axis=AX.X, op=ALU.max
+                    )
+                return
             x = work.tile([P, L], F32, name="x", tag="x")
             x_tiles[t] = x
             for half in range(2):
-                cols = slice(512 * half, 512 * half + 512)
-                nc.vector.tensor_tensor(
-                    out=x[:, cols].rearrange("p (xo rr xi) -> p xo rr xi", xo=4, rr=16, xi=8),
-                    in0=s_tiles[(t, half)][:].rearrange("p (xo rr xi) -> p xo rr xi", xo=4, rr=16, xi=8),
-                    in1=mask_sb[t][:, cols].rearrange("p (rr xo xi) -> p xo rr xi", rr=16, xo=4, xi=8),
-                    op=ALU.add,
+                cols = slice(HALF * half, HALF * half + HALF)
+                nc.vector.scalar_tensor_tensor(
+                    out=x[:, cols],
+                    in0=s_tiles[(t, half)][:],
+                    scalar=INV_SCALE,
+                    in1=mask_sb[t][:, cols],
+                    op0=ALU.mult,
+                    op1=ALU.add,
                 )
 
         def row_max(t):
             negs[t] = stat.tile([P, 1], F32, name="neg_max", tag="neg_max")
-            nc.vector.tensor_reduce(out=negs[t][:], in_=x_tiles[t][:], axis=AX.X, op=ALU.max, negate=True)
+            if t in MASK_ON_TENSOR:
+                top = stat.tile([P, 1], F32, name="top", tag="top")
+                nc.vector.tensor_reduce(out=top[:], in_=halves[t][:], axis=AX.X, op=ALU.max)
+                nc.vector.tensor_scalar(
+                    out=negs[t][:], in0=top[:], scalar1=-INV_SCALE, scalar2=None, op0=ALU.mult
+                )
+            else:
+                nc.vector.tensor_reduce(out=negs[t][:], in_=x_tiles[t][:], axis=AX.X, op=ALU.max, negate=True)
 
         def exponent(t):
-            e_tiles[t] = work.tile([P, L], BF16, name="e_sb", tag="e_sb")
+            e_sb = work.tile([P, 4, 32, 8], BF16, name="e_sb", tag="e_sb")
+            e_tiles[t] = e_sb
+            if t in MASK_ON_TENSOR:
+                sums[t] = stat.tile([P, 2], F32, name="half_sum", tag="half_sum")
+                for half in range(2):
+                    nc.scalar.activation(
+                        out=e_sb[:, :, 16 * half : 16 * half + 16, :].rearrange("p xo r xi -> p r xo xi"),
+                        in_=s_tiles[(t, half)][:].rearrange("p (r xo xi) -> p r xo xi", r=16, xo=4, xi=8),
+                        func=ACT.Exp,
+                        bias=negs[t][:, 0:1],
+                        scale=INV_SCALE,
+                        accum_out=sums[t][:, half : half + 1],
+                    )
+                return
             sums[t] = stat.tile([P, 1], F32, name="row_sum", tag="row_sum")
             nc.scalar.activation(
-                out=e_tiles[t][:],
-                in_=x_tiles[t][:],
+                out=e_sb[:].rearrange("p xo r xi -> p r xo xi"),
+                in_=x_tiles[t][:].rearrange("p (r xo xi) -> p r xo xi", r=32, xo=4, xi=8),
                 func=ACT.Exp,
                 bias=negs[t][:, 0:1],
                 scale=1.0,
                 accum_out=sums[t][:, 0:1],
             )
 
+        def flip_e(t):
+            e_t = ps_e.tile([P, 2, 4, P], BF16, name="e_t", tag="e_t")
+            et_tiles[t] = e_t
+            for g in range(2):
+                for j in range(4):
+                    nc.tensor.transpose(
+                        out=e_t[:, g, j, :],
+                        in_=e_tiles[t][:, j, 16 * g : 16 * g + 16, :].rearrange("p r xi -> p (r xi)"),
+                        identity=ident_b[:],
+                    )
+
         def reciprocal(t):
             recips[t] = stat.tile([P, 1], F32, name="recip", tag="recip")
-            nc.vector.reciprocal(out=recips[t][:], in_=sums[t][:])
+            total = sums[t]
+            if t in MASK_ON_TENSOR:
+                total = stat.tile([P, 1], F32, name="row_sum2", tag="row_sum2")
+                nc.vector.tensor_reduce(out=total[:], in_=sums[t][:], axis=AX.X, op=ALU.add)
+            nc.vector.reciprocal(out=recips[t][:], in_=total[:])
 
-        def regroup(t):
-            g_tiles[t] = work.tile([P, 2, P, 4], BF16, name="grouped", tag="grouped", align_bytes=64)
-            src = et_tiles[t][:].rearrange("p (g j) q -> p g q j", g=2, j=4)
-            if t in (NT - 3, NT - 2):
+        def leave_psum(t):
+            if t < LAST_VIA_GPSIMD:
+                lin_tiles[t] = work.tile([P, 2, 4, P], BF16, name="e_lin", tag="e_lin")
+                nc.scalar.copy(out=lin_tiles[t][:], in_=et_tiles[t][:])
+                return
+            g_tiles[t] = work.tile([P, 2, P, 4], BF16, name="grouped_end", tag="grouped_end", align_bytes=64)
+            src = et_tiles[t][:].rearrange("p g j q -> p g q j")
+            if t < NT - 1:
                 nc.vector.tensor_copy(out=g_tiles[t][:], in_=src)
             else:
                 nc.scalar.copy(out=g_tiles[t][:], in_=src)
+
+        def regroup(t):
+            g_tiles[t] = work.tile([P, 2, P, 4], BF16, name="grouped", tag="grouped", bufs=1, align_bytes=64)
+            nc.gpsimd.tensor_scalar(
+                out=g_tiles[t][:],
+                in0=lin_tiles[t][:].rearrange("p g j q -> p g q j"),
+                scalar1=1.0,
+                scalar2=0.0,
+                op0=ALU.mult,
+                op1=ALU.add,
+            )
 
         def quantise_e(t):
             codes = work.tile([P, 2 * P], U32, name="codes", tag="codes", align_bytes=64)
@@ -246,7 +325,7 @@ def tile_single_head_split_window_attention_t_kernel(
 
         def finish(t, on_vector):
             win, blk = divmod(t, NBLK)
-            o_sb = work.tile([P, C], F32, name="o_sb", tag="o_sb", bufs=4)
+            o_sb = work.tile([P, C], F32, name="o_sb", tag="o_sb", bufs=6)
             if on_vector:
                 nc.vector.tensor_scalar(
                     out=o_sb[:], in0=o_tiles[t][:], scalar1=recips[t][:, 0:1], scalar2=None, op0=ALU.mult
@@ -254,74 +333,67 @@ def tile_single_head_split_window_attention_t_kernel(
             else:
                 nc.scalar.activation(out=o_sb[:], in_=o_tiles[t][:], func=ACT.Copy, scale=recips[t][:, 0:1])
             yq, xo8 = image_block(win, blk)
-            if t < SYNC_STORES_FROM:
-                nc.gpsimd.dma_start(out=o_blk[0, yq, xo8], in_=o_sb[:])
-            else:
-                nc.sync.dma_start(out=o_blk[0, yq, xo8], in_=o_sb[:])
+            nc.sync.dma_start(out=o_blk[0, yq, xo8], in_=o_sb[:])
 
         def finish_on_vector(t):
-            return t % NBLK in (6, 7, 0, 1) or t >= NT - 5
+            return t >= NT - 5
 
         def valid(t):
             return 0 <= t < NT
 
-        scale_q(0, 0, 1)
         bank = flip_pe(k_sb, 0, [0, 1, 2, 3], ps_s, "s_ps0")
-        flip_out(k_t, 0, [0, 1, 2, 3], bank, True)
+        flip_out_k(0, 0, bank, True)
         bank = flip_pe(q_sb, 0, [0], ps_s, "s_ps1")
-        flip_out(q_t, 0, [0], bank, False)
+        flip_out_q(0, [0], bank, False)
         bank = flip_pe(k_sb, 0, [4, 5, 6, 7], ps_s, "s_ps0")
-        flip_out(k_t, 0, [4, 5, 6, 7], bank, False)
-        for half in range(2):
-            for e in range(2):
-                score_mm(0, half, e)
-        scale_q(0, 1, 4)
-        scale_q(0, 4, 8)
-        group_v(0)
+        flip_out_k(0, 1, bank, False)
+        scores(0)
         bank = flip_pe(q_sb, 0, [1, 2, 3], ps_s, "s_ps1")
-        flip_out(q_t, 0, [1, 2, 3], bank, False)
+        flip_out_q(0, [1, 2, 3], bank, False)
         bank = flip_pe(q_sb, 0, [4, 5, 6, 7], ps_s, "s_ps0")
-        flip_out(q_t, 0, [4, 5, 6, 7], bank, False)
+        flip_out_q(0, [4, 5, 6, 7], bank, False)
+        for piece in range(4):
+            group_v(0, piece)
 
-        flips = {3: (k_sb, k_t, [0, 1, 2, 3]), 4: (k_sb, k_t, [4, 5, 6, 7]), 5: (q_sb, q_t, [0, 1, 2, 3]), 6: (q_sb, q_t, [4, 5, 6, 7])}
-
-        for tau in range(NT + 5):
+        for tau in range(NT + 6):
             win, blk = divmod(tau, NBLK)
             nxt = win + 1
             prep = nxt < NWIN
-            if prep and blk == 2:
-                for lo in range(0, NBLK, 2):
-                    scale_q(nxt, lo, lo + 2)
-                group_v(nxt)
-            if valid(tau + 1):
-                for half in range(2):
-                    for e in range(2):
-                        score_mm(tau + 1, half, e)
+            load_round(ROUNDS_AHEAD + tau)
             if valid(tau - 1):
                 exponent(tau - 1)
+            if valid(tau - 6) and not finish_on_vector(tau - 6):
+                finish(tau - 6, False)
+            if valid(tau + 1):
+                scores(tau + 1)
             if valid(tau - 2):
-                flip_e(tau - 2, 0, 8)
+                flip_e(tau - 2)
             bank = None
-            if prep and blk in flips:
-                bank = flip_pe(flips[blk][0], nxt, flips[blk][2], ps_m, "misc")
+            if prep and blk in (4, 5):
+                bank = flip_pe(k_sb, nxt, [4 * (blk - 4) + i for i in range(4)], ps_m, "misc")
+            if prep and blk in (6, 7):
+                bank = flip_pe(q_sb, nxt, [4 * (blk - 6) + i for i in range(4)], ps_m, "misc")
             if valid(tau):
                 add_mask(tau)
-            if valid(tau - 5) and finish_on_vector(tau - 5):
-                finish(tau - 5, True)
-            if valid(tau - 4):
-                quantise_e(tau - 4)
-                weighted_sum(tau - 4)
+            if valid(tau - 6) and finish_on_vector(tau - 6):
+                finish(tau - 6, True)
+            if valid(tau - 5):
+                quantise_e(tau - 5)
+                weighted_sum(tau - 5)
+            if 0 <= tau - 4 < LAST_VIA_GPSIMD:
+                regroup(tau - 4)
+            v_win, v_piece = divmod(tau + 2, NBLK)
+            if 1 <= v_win < NWIN and v_piece < 4:
+                group_v(v_win, v_piece)
             if valid(tau - 2):
                 reciprocal(tau - 2)
-            if tau == 1:
-                quantise_v(0)
-            if prep and blk == 6:
-                quantise_v(nxt)
+            if win < NWIN and blk == 3:
+                quantise_v(win)
             if valid(tau):
                 row_max(tau)
             if valid(tau - 3):
-                regroup(tau - 3)
-            if bank is not None:
-                flip_out(flips[blk][1], nxt, flips[blk][2], bank, False)
-            if valid(tau - 5) and not finish_on_vector(tau - 5):
-                finish(tau - 5, False)
+                leave_psum(tau - 3)
+            if bank is not None and blk in (4, 5):
+                flip_out_k(nxt, blk - 4, bank, False)
+            if bank is not None and blk in (6, 7):
+                flip_out_q(nxt, [4 * (blk - 6) + i for i in range(4)], bank, False)

@@ -24,7 +24,6 @@ NT = NWIN * NBLK
 MASK_ON_TENSOR = tuple(range(2, NT, 5))
 FIRST_ROUND_MASK = 3
 ROUNDS_AHEAD = 4
-LAST_VIA_GPSIMD = NT - 3
 INV_SCALE = 0.0625
 
 
@@ -141,19 +140,20 @@ def tile_single_head_split_window_attention_t_kernel(
 
         v_grouped = {}
 
-        def group_v(win, piece):
-            if piece == 0:
-                v_grouped[win] = work.tile([P, 2, C, 4], BF16, name="vg", tag="vg", bufs=2, align_bytes=64)
-            g, lo = divmod(piece, 2)
+        def group_v(win):
+            vg = work.tile([P, 2, C, 4], BF16, name="vg", tag="vg", bufs=2, align_bytes=64)
             src = v_sb[win][:].rearrange("p (g j) c -> p g c j", g=2, j=4)
-            nc.gpsimd.tensor_scalar(
-                out=v_grouped[win][:, g, P * lo : P * lo + P, :],
-                in0=src[:, g, P * lo : P * lo + P, :],
-                scalar1=1.0,
-                scalar2=0.0,
-                op0=ALU.mult,
-                op1=ALU.add,
-            )
+            for g in range(2):
+                for lo in range(0, C, P):
+                    nc.gpsimd.tensor_scalar(
+                        out=vg[:, g, lo : lo + P, :],
+                        in0=src[:, g, lo : lo + P, :],
+                        scalar1=1.0,
+                        scalar2=0.0,
+                        op0=ALU.mult,
+                        op1=ALU.add,
+                    )
+            v_grouped[win] = vg
 
         def quantise_v(win):
             nc.vector.quantize_mx(
@@ -168,7 +168,6 @@ def tile_single_head_split_window_attention_t_kernel(
         e_tiles = {}
         et_tiles = {}
         g_tiles = {}
-        lin_tiles = {}
         c_tiles = {}
         o_tiles = {}
         sums = {}
@@ -275,28 +274,13 @@ def tile_single_head_split_window_attention_t_kernel(
                 nc.vector.tensor_reduce(out=total[:], in_=sums[t][:], axis=AX.X, op=ALU.add)
             nc.vector.reciprocal(out=recips[t][:], in_=total[:])
 
-        def leave_psum(t):
-            if t < LAST_VIA_GPSIMD:
-                lin_tiles[t] = work.tile([P, 2, 4, P], BF16, name="e_lin", tag="e_lin")
-                nc.scalar.copy(out=lin_tiles[t][:], in_=et_tiles[t][:])
-                return
-            g_tiles[t] = work.tile([P, 2, P, 4], BF16, name="grouped_end", tag="grouped_end", align_bytes=64)
+        def regroup(t):
+            g_tiles[t] = work.tile([P, 2, P, 4], BF16, name="grouped", tag="grouped", align_bytes=64)
             src = et_tiles[t][:].rearrange("p g j q -> p g q j")
-            if t < NT - 1:
+            if t in (NT - 3, NT - 2):
                 nc.vector.tensor_copy(out=g_tiles[t][:], in_=src)
             else:
                 nc.scalar.copy(out=g_tiles[t][:], in_=src)
-
-        def regroup(t):
-            g_tiles[t] = work.tile([P, 2, P, 4], BF16, name="grouped", tag="grouped", bufs=1, align_bytes=64)
-            nc.gpsimd.tensor_scalar(
-                out=g_tiles[t][:],
-                in0=lin_tiles[t][:].rearrange("p g j q -> p g q j"),
-                scalar1=1.0,
-                scalar2=0.0,
-                op0=ALU.mult,
-                op1=ALU.add,
-            )
 
         def quantise_e(t):
             codes = work.tile([P, 2 * P], U32, name="codes", tag="codes", align_bytes=64)
@@ -336,7 +320,7 @@ def tile_single_head_split_window_attention_t_kernel(
             nc.sync.dma_start(out=o_blk[0, yq, xo8], in_=o_sb[:])
 
         def finish_on_vector(t):
-            return t >= NT - 5
+            return t % NBLK in (7, 0, 1, 2) or t >= NT - 5
 
         def valid(t):
             return 0 <= t < NT
@@ -352,18 +336,17 @@ def tile_single_head_split_window_attention_t_kernel(
         flip_out_q(0, [1, 2, 3], bank, False)
         bank = flip_pe(q_sb, 0, [4, 5, 6, 7], ps_s, "s_ps0")
         flip_out_q(0, [4, 5, 6, 7], bank, False)
-        for piece in range(4):
-            group_v(0, piece)
+        group_v(0)
 
-        for tau in range(NT + 6):
+        for tau in range(NT + 5):
             win, blk = divmod(tau, NBLK)
             nxt = win + 1
             prep = nxt < NWIN
             load_round(ROUNDS_AHEAD + tau)
+            if prep and blk == 7:
+                group_v(nxt)
             if valid(tau - 1):
                 exponent(tau - 1)
-            if valid(tau - 6) and not finish_on_vector(tau - 6):
-                finish(tau - 6, False)
             if valid(tau + 1):
                 scores(tau + 1)
             if valid(tau - 2):
@@ -375,16 +358,11 @@ def tile_single_head_split_window_attention_t_kernel(
                 bank = flip_pe(q_sb, nxt, [4 * (blk - 6) + i for i in range(4)], ps_m, "misc")
             if valid(tau):
                 add_mask(tau)
-            if valid(tau - 6) and finish_on_vector(tau - 6):
-                finish(tau - 6, True)
-            if valid(tau - 5):
-                quantise_e(tau - 5)
-                weighted_sum(tau - 5)
-            if 0 <= tau - 4 < LAST_VIA_GPSIMD:
-                regroup(tau - 4)
-            v_win, v_piece = divmod(tau + 2, NBLK)
-            if 1 <= v_win < NWIN and v_piece < 4:
-                group_v(v_win, v_piece)
+            if valid(tau - 5) and finish_on_vector(tau - 5):
+                finish(tau - 5, True)
+            if valid(tau - 4):
+                quantise_e(tau - 4)
+                weighted_sum(tau - 4)
             if valid(tau - 2):
                 reciprocal(tau - 2)
             if win < NWIN and blk == 3:
@@ -392,8 +370,10 @@ def tile_single_head_split_window_attention_t_kernel(
             if valid(tau):
                 row_max(tau)
             if valid(tau - 3):
-                leave_psum(tau - 3)
+                regroup(tau - 3)
             if bank is not None and blk in (4, 5):
                 flip_out_k(nxt, blk - 4, bank, False)
             if bank is not None and blk in (6, 7):
                 flip_out_q(nxt, [4 * (blk - 6) + i for i in range(4)], bank, False)
+            if valid(tau - 5) and not finish_on_vector(tau - 5):
+                finish(tau - 5, False)

@@ -21,10 +21,20 @@ NBLK = 8
 L = 1024
 HALF = 512
 NT = NWIN * NBLK
+INV_SCALE = 0.0625
+
 MASK_ON_TENSOR = tuple(range(2, NT, 5))
+
+LAG_EXP = 1
+LAG_TRANSPOSE = 2
+LAG_RECIPROCAL = 2
+LAG_REGROUP = 3
+LAG_QUANTISE = 5
+LAG_MX = 6
+LAG_FINISH = 7
+
 FIRST_ROUND_MASK = 3
 ROUNDS_AHEAD = 4
-INV_SCALE = 0.0625
 
 
 def image_block(win, blk):
@@ -49,7 +59,7 @@ def tile_single_head_split_window_attention_t_kernel(
         ctx.enter_context(tc.manual_schedule())
         res = ctx.enter_context(tc.tile_pool(name="res", bufs=1))
         work = ctx.enter_context(tc.tile_pool(name="work", bufs=3))
-        stat = ctx.enter_context(tc.tile_pool(name="stat", bufs=8))
+        stat = ctx.enter_context(tc.tile_pool(name="stat", bufs=10))
         ps_s = ctx.enter_context(tc.psum_pool(name="ps_s", bufs=2))
         ps_e = ctx.enter_context(tc.psum_pool(name="ps_e", bufs=2))
         ps_m = ctx.enter_context(tc.psum_pool(name="ps_m", bufs=2))
@@ -76,6 +86,7 @@ def tile_single_head_split_window_attention_t_kernel(
         v_codes = [res.tile([P, 2 * C], U32, name="v_codes%d" % i, align_bytes=64) for i in range(NWIN)]
         v_scales = [res.tile([P, 2 * C], U8, name="v_scales%d" % i, align_bytes=64) for i in range(NWIN)]
         mask_sb = [res.tile([P, L], BF16, name="mask%d" % i) for i in range(NT)]
+
 
         def load_blocks(dst, src, win, lo, hi):
             for blk in range(lo, hi):
@@ -114,7 +125,8 @@ def tile_single_head_split_window_attention_t_kernel(
         for i in range(ROUNDS_AHEAD):
             load_round(i)
 
-        def flip_pe(src, win, group, pool, tag):
+
+        def transpose_blocks(src, win, group, pool, tag):
             bank = pool.tile([P, 4, P], F32, name="bank_" + tag, tag=tag)
             for i, blk in enumerate(group):
                 nc.tensor.transpose(
@@ -122,7 +134,7 @@ def tile_single_head_split_window_attention_t_kernel(
                 )
             return bank
 
-        def flip_out_q(win, group, bank, on_vector):
+        def keep_q(win, group, bank, on_vector):
             n = len(group)
             dst_ap = q_t[win][:, group[0] : group[0] + n, :]
             if on_vector:
@@ -130,7 +142,7 @@ def tile_single_head_split_window_attention_t_kernel(
             else:
                 nc.scalar.copy(out=dst_ap, in_=bank[:, 0:n, :])
 
-        def flip_out_k(win, yh, bank, on_vector):
+        def keep_k(win, yh, bank, on_vector):
             dst_ap = k_t[win][:, yh, :].rearrange("p (rr xo xi) -> p rr xo xi", rr=16, xo=4, xi=8)
             src_ap = bank[:].rearrange("p xo (rr xi) -> p rr xo xi", rr=16, xi=8)
             if on_vector:
@@ -162,6 +174,7 @@ def tile_single_head_split_window_attention_t_kernel(
                 in_=v_grouped[win][:].rearrange("p g c j -> p (g c j)"),
             )
 
+
         s_tiles = {}
         halves = {}
         x_tiles = {}
@@ -176,8 +189,8 @@ def tile_single_head_split_window_attention_t_kernel(
 
         def scores(t):
             win, blk = divmod(t, NBLK)
-            q_pair = q_t[win][:].bitcast(BF16).rearrange("p b (t e) -> p b t e", e=2)
-            k_pair = k_t[win][:].bitcast(BF16).rearrange("p y (t e) -> p y t e", e=2)
+            q_pair = q_t[win][:].bitcast(BF16).rearrange("p b (n e) -> p b n e", e=2)
+            k_pair = k_t[win][:].bitcast(BF16).rearrange("p y (n e) -> p y n e", e=2)
             for half in range(2):
                 s_ps = ps_s.tile([P, HALF], F32, name="s_ps%d" % half, tag="s_ps%d" % half)
                 s_tiles[(t, half)] = s_ps
@@ -255,7 +268,7 @@ def tile_single_head_split_window_attention_t_kernel(
                 accum_out=sums[t][:, 0:1],
             )
 
-        def flip_e(t):
+        def transpose_e(t):
             e_t = ps_e.tile([P, 2, 4, P], BF16, name="e_t", tag="e_t")
             et_tiles[t] = e_t
             for g in range(2):
@@ -275,9 +288,9 @@ def tile_single_head_split_window_attention_t_kernel(
             nc.vector.reciprocal(out=recips[t][:], in_=total[:])
 
         def regroup(t):
-            g_tiles[t] = work.tile([P, 2, P, 4], BF16, name="grouped", tag="grouped", align_bytes=64)
+            g_tiles[t] = work.tile([P, 2, P, 4], BF16, name="grouped", tag="grouped", bufs=4, align_bytes=64)
             src = et_tiles[t][:].rearrange("p g j q -> p g q j")
-            if t in (NT - 3, NT - 2):
+            if t == NT - 3:
                 nc.vector.tensor_copy(out=g_tiles[t][:], in_=src)
             else:
                 nc.scalar.copy(out=g_tiles[t][:], in_=src)
@@ -319,61 +332,61 @@ def tile_single_head_split_window_attention_t_kernel(
             yq, xo8 = image_block(win, blk)
             nc.sync.dma_start(out=o_blk[0, yq, xo8], in_=o_sb[:])
 
-        def finish_on_vector(t):
-            return t % NBLK in (7, 0, 1, 2) or t >= NT - 5
-
         def valid(t):
             return 0 <= t < NT
 
-        bank = flip_pe(k_sb, 0, [0, 1, 2, 3], ps_s, "s_ps0")
-        flip_out_k(0, 0, bank, True)
-        bank = flip_pe(q_sb, 0, [0], ps_s, "s_ps1")
-        flip_out_q(0, [0], bank, False)
-        bank = flip_pe(k_sb, 0, [4, 5, 6, 7], ps_s, "s_ps0")
-        flip_out_k(0, 1, bank, False)
+        bank = transpose_blocks(k_sb, 0, [0, 1, 2, 3], ps_s, "s_ps0")
+        keep_k(0, 0, bank, True)
+        bank = transpose_blocks(q_sb, 0, [0], ps_s, "s_ps1")
+        keep_q(0, [0], bank, False)
+        bank = transpose_blocks(k_sb, 0, [4, 5, 6, 7], ps_s, "s_ps0")
+        keep_k(0, 1, bank, False)
         scores(0)
-        bank = flip_pe(q_sb, 0, [1, 2, 3], ps_s, "s_ps1")
-        flip_out_q(0, [1, 2, 3], bank, False)
-        bank = flip_pe(q_sb, 0, [4, 5, 6, 7], ps_s, "s_ps0")
-        flip_out_q(0, [4, 5, 6, 7], bank, False)
+        bank = transpose_blocks(q_sb, 0, [1, 2, 3], ps_s, "s_ps1")
+        keep_q(0, [1, 2, 3], bank, False)
+        bank = transpose_blocks(q_sb, 0, [4, 5, 6, 7], ps_s, "s_ps0")
+        keep_q(0, [4, 5, 6, 7], bank, False)
         group_v(0)
 
-        for tau in range(NT + 5):
+        for tau in range(NT + LAG_FINISH):
             win, blk = divmod(tau, NBLK)
             nxt = win + 1
-            prep = nxt < NWIN
+            prepare = nxt < NWIN
+            part = blk - 4
+            group = [4 * (part % 2) + i for i in range(4)]
+            last = tau - LAG_FINISH
+            last_on_vector = blk >= 4 or last >= NT - 5
+
             load_round(ROUNDS_AHEAD + tau)
-            if prep and blk == 7:
+            if prepare and blk == 7:
                 group_v(nxt)
-            if valid(tau - 1):
-                exponent(tau - 1)
+            if valid(tau - LAG_EXP):
+                exponent(tau - LAG_EXP)
             if valid(tau + 1):
                 scores(tau + 1)
-            if valid(tau - 2):
-                flip_e(tau - 2)
-            bank = None
-            if prep and blk in (4, 5):
-                bank = flip_pe(k_sb, nxt, [4 * (blk - 4) + i for i in range(4)], ps_m, "misc")
-            if prep and blk in (6, 7):
-                bank = flip_pe(q_sb, nxt, [4 * (blk - 6) + i for i in range(4)], ps_m, "misc")
+            if valid(tau - LAG_TRANSPOSE):
+                transpose_e(tau - LAG_TRANSPOSE)
+            if prepare and part >= 0:
+                bank = transpose_blocks(k_sb if part < 2 else q_sb, nxt, group, ps_m, "misc")
             if valid(tau):
                 add_mask(tau)
-            if valid(tau - 5) and finish_on_vector(tau - 5):
-                finish(tau - 5, True)
-            if valid(tau - 4):
-                quantise_e(tau - 4)
-                weighted_sum(tau - 4)
-            if valid(tau - 2):
-                reciprocal(tau - 2)
+            if valid(last) and last_on_vector:
+                finish(last, True)
+            if valid(tau - LAG_MX):
+                weighted_sum(tau - LAG_MX)
+            if valid(tau - LAG_QUANTISE):
+                quantise_e(tau - LAG_QUANTISE)
+            if valid(tau - LAG_RECIPROCAL):
+                reciprocal(tau - LAG_RECIPROCAL)
             if win < NWIN and blk == 3:
                 quantise_v(win)
             if valid(tau):
                 row_max(tau)
-            if valid(tau - 3):
-                regroup(tau - 3)
-            if bank is not None and blk in (4, 5):
-                flip_out_k(nxt, blk - 4, bank, False)
-            if bank is not None and blk in (6, 7):
-                flip_out_q(nxt, [4 * (blk - 6) + i for i in range(4)], bank, False)
-            if valid(tau - 5) and not finish_on_vector(tau - 5):
-                finish(tau - 5, False)
+            if valid(tau - LAG_REGROUP):
+                regroup(tau - LAG_REGROUP)
+            if prepare and 0 <= part < 2:
+                keep_k(nxt, part, bank, False)
+            if prepare and part >= 2:
+                keep_q(nxt, group, bank, False)
+            if valid(last) and not last_on_vector:
+                finish(last, False)

@@ -51,7 +51,7 @@ def tile_single_head_split_window_attention_t_kernel(
     blocks = "o (yq rr xo xi) c -> o yq xo rr xi c"
     q_blk = q.rearrange(blocks, yq=4, rr=16, xo=8, xi=8)
     k_blk = k.rearrange(blocks, yq=4, rr=16, xo=8, xi=8)
-    v_blk = v.rearrange(blocks, yq=4, rr=16, xo=8, xi=8)
+    v_blk = v.rearrange("o (yq rr xq p8 e) c -> o yq xq rr p8 (e c)", yq=4, rr=16, xq=4, p8=8, e=2)
     o_blk = out.rearrange(blocks, yq=4, rr=16, xo=8, xi=8)
     m_blk = attn_mask.rearrange("j (yh rr xo xi) n -> j yh xo rr xi n", yh=2, rr=16, xo=4, xi=8)
 
@@ -93,6 +93,15 @@ def tile_single_head_split_window_attention_t_kernel(
                 yq, xo8 = image_block(win, blk)
                 nc.sync.dma_start(out=dst[win][:, blk, :], in_=src[0, yq, xo8])
 
+        def load_v(win, lo, hi):
+            wy, wx = divmod(win, 2)
+            for piece in range(lo, hi):
+                g, u = divmod(piece, 2)
+                nc.sync.dma_start(
+                    out=v_sb[win][:, 2 * piece : 2 * piece + 2, :].rearrange("p j c -> p (j c)"),
+                    in_=v_blk[0, (2 * wy + g + 1) % 4, (2 * wx + u + 1) % 4],
+                )
+
         def load_masks(lo, hi):
             for t in range(lo, hi):
                 win, blk = divmod(t, NBLK)
@@ -107,11 +116,11 @@ def tile_single_head_split_window_attention_t_kernel(
         load_masks(1, 2)
         load_blocks(q_sb, q_blk, 0, 4, 8)
         load_masks(2, 3)
-        load_blocks(v_sb, v_blk, 0, 0, 8)
+        load_v(0, 0, 4)
 
         later = []
         for win in range(1, NWIN):
-            for dst, src in ((k_sb, k_blk), (q_sb, q_blk), (v_sb, v_blk)):
+            for dst, src in ((k_sb, k_blk), (q_sb, q_blk), (v_sb, None)):
                 for lo in range(0, NBLK, 4):
                     later.append((dst, src, win, lo))
 
@@ -120,7 +129,10 @@ def tile_single_head_split_window_attention_t_kernel(
                 load_masks(FIRST_ROUND_MASK + i, FIRST_ROUND_MASK + i + 1)
             if i < len(later):
                 dst, src, win, lo = later[i]
-                load_blocks(dst, src, win, lo, lo + 4)
+                if src is None:
+                    load_v(win, lo // 2, lo // 2 + 2)
+                else:
+                    load_blocks(dst, src, win, lo, lo + 4)
 
         for i in range(ROUNDS_AHEAD):
             load_round(i)
@@ -244,14 +256,14 @@ def tile_single_head_split_window_attention_t_kernel(
                 nc.vector.tensor_reduce(out=negs[t][:], in_=x_tiles[t][:], axis=AX.X, op=ALU.max, negate=True)
 
         def exponent(t):
-            e_sb = work.tile([P, 4, 32, 8], BF16, name="e_sb", tag="e_sb")
+            e_sb = work.tile([P, 2, 32, 16], BF16, name="e_sb", tag="e_sb")
             e_tiles[t] = e_sb
             if t in MASK_ON_TENSOR:
                 sums[t] = stat.tile([P, 2], F32, name="half_sum", tag="half_sum")
                 for half in range(2):
                     nc.scalar.activation(
-                        out=e_sb[:, :, 16 * half : 16 * half + 16, :].rearrange("p xo r xi -> p r xo xi"),
-                        in_=s_tiles[(t, half)][:].rearrange("p (r xo xi) -> p r xo xi", r=16, xo=4, xi=8),
+                        out=e_sb[:, :, 16 * half : 16 * half + 16, :].rearrange("p u r w -> p r u w"),
+                        in_=s_tiles[(t, half)][:].rearrange("p (r u w) -> p r u w", r=16, u=2, w=16),
                         func=ACT.Exp,
                         bias=negs[t][:, 0:1],
                         scale=INV_SCALE,
@@ -260,8 +272,8 @@ def tile_single_head_split_window_attention_t_kernel(
                 return
             sums[t] = stat.tile([P, 1], F32, name="row_sum", tag="row_sum")
             nc.scalar.activation(
-                out=e_sb[:].rearrange("p xo r xi -> p r xo xi"),
-                in_=x_tiles[t][:].rearrange("p (r xo xi) -> p r xo xi", r=32, xo=4, xi=8),
+                out=e_sb[:].rearrange("p u r w -> p r u w"),
+                in_=x_tiles[t][:].rearrange("p (r u w) -> p r u w", r=32, u=2, w=16),
                 func=ACT.Exp,
                 bias=negs[t][:, 0:1],
                 scale=1.0,
@@ -269,14 +281,14 @@ def tile_single_head_split_window_attention_t_kernel(
             )
 
         def transpose_e(t):
-            e_t = ps_e.tile([P, 2, 4, P], BF16, name="e_t", tag="e_t")
+            e_t = ps_e.tile([P, 2, 2, P], F32, name="e_t", tag="e_t")
             et_tiles[t] = e_t
             for g in range(2):
-                for j in range(4):
+                for u in range(2):
                     nc.tensor.transpose(
-                        out=e_t[:, g, j, :],
-                        in_=e_tiles[t][:, j, 16 * g : 16 * g + 16, :].rearrange("p r xi -> p (r xi)"),
-                        identity=ident_b[:],
+                        out=e_t[:, g, u, :],
+                        in_=e_tiles[t][:, u, 16 * g : 16 * g + 16, :].rearrange("p r w -> p (r w)").bitcast(F32),
+                        identity=ident_f[:],
                     )
 
         def reciprocal(t):
@@ -289,11 +301,12 @@ def tile_single_head_split_window_attention_t_kernel(
 
         def regroup(t):
             g_tiles[t] = work.tile([P, 2, P, 4], BF16, name="grouped", tag="grouped", bufs=4, align_bytes=64)
-            src = et_tiles[t][:].rearrange("p g j q -> p g q j")
+            src = et_tiles[t][:].rearrange("p g u q -> p g q u")
+            dst = g_tiles[t][:].rearrange("p g q j -> p g (q j)").bitcast(F32).rearrange("p g (q u) -> p g q u", u=2)
             if t == NT - 3:
-                nc.vector.tensor_copy(out=g_tiles[t][:], in_=src)
+                nc.vector.tensor_copy(out=dst, in_=src)
             else:
-                nc.scalar.copy(out=g_tiles[t][:], in_=src)
+                nc.scalar.copy(out=dst, in_=src)
 
         def quantise_e(t):
             codes = work.tile([P, 2 * P], U32, name="codes", tag="codes", align_bytes=64)

@@ -27,11 +27,14 @@ MASK_ON_TENSOR = tuple(range(2, NT, 5))
 
 LAG_EXP = 1
 LAG_TRANSPOSE = 2
-LAG_RECIPROCAL = 2
+LAG_JOIN = 2
 LAG_REGROUP = 3
 LAG_QUANTISE = 5
 LAG_MX = 6
 LAG_FINISH = 7
+
+GROUP = 4
+LAG_RECIPROCAL = 6
 
 FIRST_ROUND_MASK = 3
 ROUNDS_AHEAD = 4
@@ -198,6 +201,13 @@ def tile_single_head_split_window_attention_t_kernel(
         sums = {}
         negs = {}
         recips = {}
+        sum_groups = {}
+
+        def sum_column(t):
+            grp, col = divmod(t, GROUP)
+            if grp not in sum_groups:
+                sum_groups[grp] = stat.tile([P, GROUP], F32, name="row_sums", tag="row_sums")
+            return sum_groups[grp][:, col : col + 1]
 
         def scores(t):
             win, blk = divmod(t, NBLK)
@@ -247,10 +257,13 @@ def tile_single_head_split_window_attention_t_kernel(
         def row_max(t):
             negs[t] = stat.tile([P, 1], F32, name="neg_max", tag="neg_max")
             if t in MASK_ON_TENSOR:
-                top = stat.tile([P, 1], F32, name="top", tag="top")
-                nc.vector.tensor_reduce(out=top[:], in_=halves[t][:], axis=AX.X, op=ALU.max)
                 nc.vector.tensor_scalar(
-                    out=negs[t][:], in0=top[:], scalar1=-INV_SCALE, scalar2=None, op0=ALU.mult
+                    out=negs[t][:],
+                    in0=halves[t][:, 0:1],
+                    scalar1=halves[t][:, 1:2],
+                    scalar2=-INV_SCALE,
+                    op0=ALU.max,
+                    op1=ALU.mult,
                 )
             else:
                 nc.vector.tensor_reduce(out=negs[t][:], in_=x_tiles[t][:], axis=AX.X, op=ALU.max, negate=True)
@@ -270,14 +283,13 @@ def tile_single_head_split_window_attention_t_kernel(
                         accum_out=sums[t][:, half : half + 1],
                     )
                 return
-            sums[t] = stat.tile([P, 1], F32, name="row_sum", tag="row_sum")
             nc.scalar.activation(
                 out=e_sb[:].rearrange("p u r w -> p r u w"),
                 in_=x_tiles[t][:].rearrange("p (r u w) -> p r u w", r=32, u=2, w=16),
                 func=ACT.Exp,
                 bias=negs[t][:, 0:1],
                 scale=1.0,
-                accum_out=sums[t][:, 0:1],
+                accum_out=sum_column(t),
             )
 
         def transpose_e(t):
@@ -291,13 +303,12 @@ def tile_single_head_split_window_attention_t_kernel(
                         identity=ident_f[:],
                     )
 
-        def reciprocal(t):
-            recips[t] = stat.tile([P, 1], F32, name="recip", tag="recip")
-            total = sums[t]
-            if t in MASK_ON_TENSOR:
-                total = stat.tile([P, 1], F32, name="row_sum2", tag="row_sum2")
-                nc.vector.tensor_reduce(out=total[:], in_=sums[t][:], axis=AX.X, op=ALU.add)
-            nc.vector.reciprocal(out=recips[t][:], in_=total[:])
+        def join_sums(t):
+            nc.vector.tensor_reduce(out=sum_column(t), in_=sums[t][:], axis=AX.X, op=ALU.add)
+
+        def reciprocal(grp):
+            recips[grp] = stat.tile([P, GROUP], F32, name="recip", tag="recip")
+            nc.vector.reciprocal(out=recips[grp][:], in_=sum_groups[grp][:])
 
         def regroup(t):
             g_tiles[t] = work.tile([P, 2, P, 4], BF16, name="grouped", tag="grouped", bufs=4, align_bytes=64)
@@ -336,12 +347,13 @@ def tile_single_head_split_window_attention_t_kernel(
         def finish(t, on_vector):
             win, blk = divmod(t, NBLK)
             o_sb = work.tile([P, C], F32, name="o_sb", tag="o_sb", bufs=6)
+            recip = recips[t // GROUP][:, t % GROUP : t % GROUP + 1]
             if on_vector:
                 nc.vector.tensor_scalar(
-                    out=o_sb[:], in0=o_tiles[t][:], scalar1=recips[t][:, 0:1], scalar2=None, op0=ALU.mult
+                    out=o_sb[:], in0=o_tiles[t][:], scalar1=recip, scalar2=None, op0=ALU.mult
                 )
             else:
-                nc.scalar.activation(out=o_sb[:], in_=o_tiles[t][:], func=ACT.Copy, scale=recips[t][:, 0:1])
+                nc.scalar.activation(out=o_sb[:], in_=o_tiles[t][:], func=ACT.Copy, scale=recip)
             yq, xo8 = image_block(win, blk)
             nc.sync.dma_start(out=o_blk[0, yq, xo8], in_=o_sb[:])
 
@@ -368,11 +380,13 @@ def tile_single_head_split_window_attention_t_kernel(
             part = blk - 4
             group = [4 * (part % 2) + i for i in range(4)]
             last = tau - LAG_FINISH
-            last_on_vector = blk >= 4 or last >= NT - 5
+            last_on_vector = last >= NT - 5
 
             load_round(ROUNDS_AHEAD + tau)
             if prepare and blk == 7:
                 group_v(nxt)
+            if valid(last) and not last_on_vector:
+                finish(last, False)
             if valid(tau - LAG_EXP):
                 exponent(tau - LAG_EXP)
             if valid(tau + 1):
@@ -389,8 +403,10 @@ def tile_single_head_split_window_attention_t_kernel(
                 weighted_sum(tau - LAG_MX)
             if valid(tau - LAG_QUANTISE):
                 quantise_e(tau - LAG_QUANTISE)
-            if valid(tau - LAG_RECIPROCAL):
-                reciprocal(tau - LAG_RECIPROCAL)
+            if tau - LAG_JOIN in MASK_ON_TENSOR:
+                join_sums(tau - LAG_JOIN)
+            if valid(tau - LAG_RECIPROCAL) and (tau - LAG_RECIPROCAL) % GROUP == 0:
+                reciprocal((tau - LAG_RECIPROCAL) // GROUP)
             if win < NWIN and blk == 3:
                 quantise_v(win)
             if valid(tau):
@@ -401,5 +417,3 @@ def tile_single_head_split_window_attention_t_kernel(
                 keep_k(nxt, part, bank, False)
             if prepare and part >= 2:
                 keep_q(nxt, group, bank, False)
-            if valid(last) and not last_on_vector:
-                finish(last, False)

@@ -209,29 +209,32 @@ def tile_single_head_split_window_attention_t_kernel(
                 sum_groups[grp] = stat.tile([P, GROUP], F32, name="row_sums", tag="row_sums")
             return sum_groups[grp][:, col : col + 1]
 
-        def scores(t):
+        def scores_half(t, half):
             win, blk = divmod(t, NBLK)
             q_pair = q_t[win][:].bitcast(BF16).rearrange("p b (n e) -> p b n e", e=2)
             k_pair = k_t[win][:].bitcast(BF16).rearrange("p y (n e) -> p y n e", e=2)
-            for half in range(2):
-                s_ps = ps_s.tile([P, HALF], F32, name="s_ps%d" % half, tag="s_ps%d" % half)
-                s_tiles[(t, half)] = s_ps
-                for e in range(2):
-                    nc.tensor.matmul(
-                        out=s_ps[:],
-                        lhsT=q_pair[:, blk, :, e],
-                        rhs=k_pair[:, half, :, e],
-                        start=(e == 0),
-                        stop=(e == 1 and t not in MASK_ON_TENSOR),
-                    )
-                if t in MASK_ON_TENSOR:
-                    nc.tensor.matmul(
-                        out=s_ps[:],
-                        lhsT=ident_16[:],
-                        rhs=mask_sb[t][:, HALF * half : HALF * half + HALF],
-                        start=False,
-                        stop=True,
-                    )
+            s_ps = ps_s.tile([P, HALF], F32, name="s_ps%d" % half, tag="s_ps%d" % half)
+            s_tiles[(t, half)] = s_ps
+            for e in range(2):
+                nc.tensor.matmul(
+                    out=s_ps[:],
+                    lhsT=q_pair[:, blk, :, e],
+                    rhs=k_pair[:, half, :, e],
+                    start=(e == 0),
+                    stop=(e == 1 and t not in MASK_ON_TENSOR),
+                )
+            if t in MASK_ON_TENSOR:
+                nc.tensor.matmul(
+                    out=s_ps[:],
+                    lhsT=ident_16[:],
+                    rhs=mask_sb[t][:, HALF * half : HALF * half + HALF],
+                    start=False,
+                    stop=True,
+                )
+
+        def scores(t):
+            scores_half(t, 0)
+            scores_half(t, 1)
 
         def add_mask(t):
             if t in MASK_ON_TENSOR:
@@ -369,6 +372,7 @@ def tile_single_head_split_window_attention_t_kernel(
         scores(0)
         bank = transpose_blocks(q_sb, 0, [1, 2, 3], ps_s, "s_ps1")
         keep_q(0, [1, 2, 3], bank, False)
+        scores(1)
         bank = transpose_blocks(q_sb, 0, [4, 5, 6, 7], ps_s, "s_ps0")
         keep_q(0, [4, 5, 6, 7], bank, False)
         group_v(0)
@@ -377,7 +381,7 @@ def tile_single_head_split_window_attention_t_kernel(
             win, blk = divmod(tau, NBLK)
             nxt = win + 1
             prepare = nxt < NWIN
-            part = blk - 4
+            part = blk - 3
             group = [4 * (part % 2) + i for i in range(4)]
             last = tau - LAG_FINISH
             last_on_vector = last >= NT - 5
@@ -387,20 +391,23 @@ def tile_single_head_split_window_attention_t_kernel(
                 group_v(nxt)
             if valid(last) and not last_on_vector:
                 finish(last, False)
-            if valid(tau - LAG_EXP):
+            if valid(tau - LAG_EXP) and tau - LAG_EXP not in MASK_ON_TENSOR:
                 exponent(tau - LAG_EXP)
-            if valid(tau + 1):
-                scores(tau + 1)
+            if valid(tau - LAG_MX) and not valid(tau + 2):
+                weighted_sum(tau - LAG_MX)
             if valid(tau - LAG_TRANSPOSE):
                 transpose_e(tau - LAG_TRANSPOSE)
-            if prepare and part >= 0:
+            if prepare and 0 <= part < 4:
                 bank = transpose_blocks(k_sb if part < 2 else q_sb, nxt, group, ps_m, "misc")
             if valid(tau):
                 add_mask(tau)
             if valid(last) and last_on_vector:
                 finish(last, True)
-            if valid(tau - LAG_MX):
-                weighted_sum(tau - LAG_MX)
+            if valid(tau + 2):
+                scores_half(tau + 2, 0)
+                if valid(tau - LAG_MX):
+                    weighted_sum(tau - LAG_MX)
+                scores_half(tau + 2, 1)
             if valid(tau - LAG_QUANTISE):
                 quantise_e(tau - LAG_QUANTISE)
             if tau - LAG_JOIN in MASK_ON_TENSOR:
@@ -413,7 +420,9 @@ def tile_single_head_split_window_attention_t_kernel(
                 row_max(tau)
             if valid(tau - LAG_REGROUP):
                 regroup(tau - LAG_REGROUP)
+            if tau in MASK_ON_TENSOR:
+                exponent(tau)
             if prepare and 0 <= part < 2:
                 keep_k(nxt, part, bank, False)
-            if prepare and part >= 2:
+            if prepare and 2 <= part < 4:
                 keep_q(nxt, group, bank, False)

@@ -40,10 +40,10 @@ FIRST_ROUND_MASK = 3
 ROUNDS_AHEAD = 4
 
 
-def image_block(win, blk):
+def image_slab(win, slab):
     wy, wx = divmod(win, 2)
-    yh, xo = divmod(blk, 4)
-    return (2 * wy + yh + 1) % 4, (4 * wx + xo + 2) % 8
+    g, u = divmod(slab, 2)
+    return (2 * wy + g + 1) % 4, (2 * wx + u + 1) % 4
 
 
 def tile_single_head_split_window_attention_t_kernel(
@@ -51,12 +51,12 @@ def tile_single_head_split_window_attention_t_kernel(
 ):
     nc = tc.nc
     assert (num_splits, with_shift, h, w) == (2, 1, 64, 64)
-    blocks = "o (yq rr xo xi) c -> o yq xo rr xi c"
-    q_blk = q.rearrange(blocks, yq=4, rr=16, xo=8, xi=8)
-    k_blk = k.rearrange(blocks, yq=4, rr=16, xo=8, xi=8)
-    v_blk = v.rearrange("o (yq rr xq p8 e) c -> o yq xq rr p8 (e c)", yq=4, rr=16, xq=4, p8=8, e=2)
-    o_blk = out.rearrange(blocks, yq=4, rr=16, xo=8, xi=8)
-    m_blk = attn_mask.rearrange("j (yh rr xo xi) n -> j yh xo rr xi n", yh=2, rr=16, xo=4, xi=8)
+    slabs = "o (yq rr xq x8 e) c -> o yq xq rr x8 (e c)"
+    q_slab = q.rearrange(slabs, yq=4, rr=16, xq=4, x8=8, e=2)
+    k_slab = k.rearrange(slabs, yq=4, rr=16, xq=4, x8=8, e=2)
+    v_slab = v.rearrange(slabs, yq=4, rr=16, xq=4, x8=8, e=2)
+    o_blk = out.rearrange("o (yq rr xq x8 e) c -> o yq xq e rr x8 c", yq=4, rr=16, xq=4, x8=8, e=2)
+    m_blk = attn_mask.rearrange("j (g rr u x8 e) n -> j g u e rr x8 n", g=2, rr=16, u=2, x8=8, e=2)
 
     with ExitStack() as ctx:
         ctx.enter_context(tc.manual_schedule())
@@ -91,51 +91,42 @@ def tile_single_head_split_window_attention_t_kernel(
         mask_sb = [res.tile([P, L], BF16, name="mask%d" % i) for i in range(NT)]
 
 
-        def load_blocks(dst, src, win, lo, hi):
-            for blk in range(lo, hi):
-                yq, xo8 = image_block(win, blk)
-                nc.sync.dma_start(out=dst[win][:, blk, :], in_=src[0, yq, xo8])
-
-        def load_v(win, lo, hi):
-            wy, wx = divmod(win, 2)
-            for piece in range(lo, hi):
-                g, u = divmod(piece, 2)
+        def load_slabs(dst, src, win, lo, hi):
+            for slab in range(lo, hi):
+                yq, xq = image_slab(win, slab)
                 nc.sync.dma_start(
-                    out=v_sb[win][:, 2 * piece : 2 * piece + 2, :].rearrange("p j c -> p (j c)"),
-                    in_=v_blk[0, (2 * wy + g + 1) % 4, (2 * wx + u + 1) % 4],
+                    out=dst[win][:, 2 * slab : 2 * slab + 2, :].rearrange("p j c -> p (j c)"), in_=src[0, yq, xq]
                 )
 
-        def load_masks(lo, hi):
-            for t in range(lo, hi):
-                win, blk = divmod(t, NBLK)
-                yh, xo = divmod(blk, 4)
-                nc.sync.dma_start(out=mask_sb[t][:], in_=m_blk[win, yh, xo])
+        def load_mask(t, lo, hi):
+            win, blk = divmod(t, NBLK)
+            slab, e = divmod(blk, 2)
+            g, u = divmod(slab, 2)
+            nc.sync.dma_start(out=mask_sb[t][:, lo:hi], in_=m_blk[win, g, u, e, :, :, lo:hi])
 
-        load_blocks(q_sb, q_blk, 0, 0, 1)
-        load_blocks(k_sb, k_blk, 0, 0, 4)
-        load_masks(0, 1)
-        load_blocks(k_sb, k_blk, 0, 4, 8)
-        load_blocks(q_sb, q_blk, 0, 1, 4)
-        load_masks(1, 2)
-        load_blocks(q_sb, q_blk, 0, 4, 8)
-        load_masks(2, 3)
-        load_v(0, 0, 4)
+        load_slabs(k_sb, k_slab, 0, 0, 2)
+        load_slabs(q_sb, q_slab, 0, 0, 1)
+        load_slabs(k_sb, k_slab, 0, 2, 4)
+        load_mask(0, 0, HALF)
+        load_mask(0, HALF, L)
+        load_mask(1, 0, L)
+        load_slabs(q_sb, q_slab, 0, 1, 2)
+        load_mask(2, 0, L)
+        load_slabs(q_sb, q_slab, 0, 2, 4)
+        load_slabs(v_sb, v_slab, 0, 0, 4)
 
         later = []
         for win in range(1, NWIN):
-            for dst, src in ((k_sb, k_blk), (q_sb, q_blk), (v_sb, None)):
-                for lo in range(0, NBLK, 4):
+            for dst, src in ((k_sb, k_slab), (q_sb, q_slab), (v_sb, v_slab)):
+                for lo in range(0, 4, 2):
                     later.append((dst, src, win, lo))
 
         def load_round(i):
             if FIRST_ROUND_MASK + i < NT:
-                load_masks(FIRST_ROUND_MASK + i, FIRST_ROUND_MASK + i + 1)
+                load_mask(FIRST_ROUND_MASK + i, 0, L)
             if i < len(later):
                 dst, src, win, lo = later[i]
-                if src is None:
-                    load_v(win, lo // 2, lo // 2 + 2)
-                else:
-                    load_blocks(dst, src, win, lo, lo + 4)
+                load_slabs(dst, src, win, lo, lo + 2)
 
         for i in range(ROUNDS_AHEAD):
             load_round(i)
@@ -158,8 +149,8 @@ def tile_single_head_split_window_attention_t_kernel(
                 nc.scalar.copy(out=dst_ap, in_=bank[:, 0:n, :])
 
         def keep_k(win, yh, bank, on_vector):
-            dst_ap = k_t[win][:, yh, :].rearrange("p (rr xo xi) -> p rr xo xi", rr=16, xo=4, xi=8)
-            src_ap = bank[:].rearrange("p xo (rr xi) -> p rr xo xi", rr=16, xi=8)
+            dst_ap = k_t[win][:, yh, :].rearrange("p (rr u x8 e) -> p u rr x8 e", rr=16, u=2, x8=8, e=2)
+            src_ap = bank[:].rearrange("p (u e) (rr x8) -> p u rr x8 e", u=2, e=2, rr=16, x8=8)
             if on_vector:
                 nc.vector.tensor_copy(out=dst_ap, in_=src_ap)
             else:
@@ -357,23 +348,23 @@ def tile_single_head_split_window_attention_t_kernel(
                 )
             else:
                 nc.scalar.activation(out=o_sb[:], in_=o_tiles[t][:], func=ACT.Copy, scale=recip)
-            yq, xo8 = image_block(win, blk)
-            nc.sync.dma_start(out=o_blk[0, yq, xo8], in_=o_sb[:])
+            yq, xq = image_slab(win, blk // 2)
+            nc.sync.dma_start(out=o_blk[0, yq, xq, blk % 2], in_=o_sb[:])
 
         def valid(t):
             return 0 <= t < NT
 
-        bank = transpose_blocks(k_sb, 0, [0, 1, 2, 3], ps_s, "s_ps0")
+        bank = transpose_blocks(k_sb, 0, [0, 1, 2, 3], ps_m, "misc")
         keep_k(0, 0, bank, True)
-        bank = transpose_blocks(q_sb, 0, [0], ps_s, "s_ps1")
-        keep_q(0, [0], bank, False)
-        bank = transpose_blocks(k_sb, 0, [4, 5, 6, 7], ps_s, "s_ps0")
+        bank = transpose_blocks(q_sb, 0, [0, 1], ps_m, "misc")
+        keep_q(0, [0, 1], bank, False)
+        bank = transpose_blocks(k_sb, 0, [4, 5, 6, 7], ps_e, "e_t")
         keep_k(0, 1, bank, False)
         scores(0)
-        bank = transpose_blocks(q_sb, 0, [1, 2, 3], ps_s, "s_ps1")
-        keep_q(0, [1, 2, 3], bank, False)
         scores(1)
-        bank = transpose_blocks(q_sb, 0, [4, 5, 6, 7], ps_s, "s_ps0")
+        bank = transpose_blocks(q_sb, 0, [2, 3], ps_e, "e_t")
+        keep_q(0, [2, 3], bank, False)
+        bank = transpose_blocks(q_sb, 0, [4, 5, 6, 7], ps_m, "misc")
         keep_q(0, [4, 5, 6, 7], bank, False)
         group_v(0)
 

@@ -189,7 +189,6 @@ def tile_single_head_split_window_attention_t_kernel(
         g_tiles = {}
         c_tiles = {}
         o_tiles = {}
-        sums = {}
         negs = {}
         recips = {}
         sum_groups = {}
@@ -228,61 +227,48 @@ def tile_single_head_split_window_attention_t_kernel(
             scores_half(t, 1)
 
         def add_mask(t):
-            if t in MASK_ON_TENSOR:
-                halves[t] = stat.tile([P, 2], F32, name="half_max", tag="half_max")
-                for half in range(2):
-                    nc.vector.tensor_reduce(
-                        out=halves[t][:, half : half + 1], in_=s_tiles[(t, half)][:], axis=AX.X, op=ALU.max
-                    )
-                return
             x = work.tile([P, L], F32, name="x", tag="x")
             x_tiles[t] = x
+            if t in MASK_ON_TENSOR:
+                halves[t] = stat.tile([P, 2], F32, name="half_min", tag="half_min")
             for half in range(2):
                 cols = slice(HALF * half, HALF * half + HALF)
-                nc.vector.scalar_tensor_tensor(
-                    out=x[:, cols],
-                    in0=s_tiles[(t, half)][:],
-                    scalar=INV_SCALE,
-                    in1=mask_sb[t][:, cols],
-                    op0=ALU.mult,
-                    op1=ALU.add,
-                )
+                if t in MASK_ON_TENSOR:
+                    nc.vector.tensor_scalar(
+                        out=x[:, cols],
+                        in0=s_tiles[(t, half)][:],
+                        scalar1=-INV_SCALE,
+                        scalar2=None,
+                        op0=ALU.mult,
+                        op1=ALU.min,
+                        accum_out=halves[t][:, half : half + 1],
+                    )
+                else:
+                    nc.vector.scalar_tensor_tensor(
+                        out=x[:, cols],
+                        in0=s_tiles[(t, half)][:],
+                        scalar=INV_SCALE,
+                        in1=mask_sb[t][:, cols],
+                        op0=ALU.mult,
+                        op1=ALU.add,
+                    )
 
         def row_max(t):
             negs[t] = stat.tile([P, 1], F32, name="neg_max", tag="neg_max")
             if t in MASK_ON_TENSOR:
-                nc.vector.tensor_scalar(
-                    out=negs[t][:],
-                    in0=halves[t][:, 0:1],
-                    scalar1=halves[t][:, 1:2],
-                    scalar2=-INV_SCALE,
-                    op0=ALU.max,
-                    op1=ALU.mult,
-                )
+                nc.vector.tensor_reduce(out=negs[t][:], in_=halves[t][:], axis=AX.X, op=ALU.min)
             else:
                 nc.vector.tensor_reduce(out=negs[t][:], in_=x_tiles[t][:], axis=AX.X, op=ALU.max, negate=True)
 
         def exponent(t):
             e_sb = work.tile([P, 2, 32, 16], BF16, name="e_sb", tag="e_sb")
             e_tiles[t] = e_sb
-            if t in MASK_ON_TENSOR:
-                sums[t] = stat.tile([P, 2], F32, name="half_sum", tag="half_sum")
-                for half in range(2):
-                    nc.scalar.activation(
-                        out=e_sb[:, :, 16 * half : 16 * half + 16, :].rearrange("p u r w -> p r u w"),
-                        in_=s_tiles[(t, half)][:].rearrange("p (r u w) -> p r u w", r=16, u=2, w=16),
-                        func=ACT.Exp,
-                        bias=negs[t][:, 0:1],
-                        scale=INV_SCALE,
-                        accum_out=sums[t][:, half : half + 1],
-                    )
-                return
             nc.scalar.activation(
                 out=e_sb[:].rearrange("p u r w -> p r u w"),
                 in_=x_tiles[t][:].rearrange("p (r u w) -> p r u w", r=32, u=2, w=16),
                 func=ACT.Exp,
                 bias=negs[t][:, 0:1],
-                scale=1.0,
+                scale=-1.0 if t in MASK_ON_TENSOR else 1.0,
                 accum_out=sum_column(t),
             )
 
@@ -296,9 +282,6 @@ def tile_single_head_split_window_attention_t_kernel(
                         in_=e_tiles[t][:, u, 16 * g : 16 * g + 16, :].rearrange("p r w -> p (r w)").bitcast(F32),
                         identity=ident_f[:],
                     )
-
-        def join_sums(t):
-            nc.vector.tensor_reduce(out=sum_column(t), in_=sums[t][:], axis=AX.X, op=ALU.add)
 
         def reciprocal(grp):
             recips[grp] = stat.tile([P, GROUP], F32, name="recip", tag="recip")
@@ -382,7 +365,7 @@ def tile_single_head_split_window_attention_t_kernel(
                 group_v(nxt)
             if valid(last) and not last_on_vector:
                 finish(last, False)
-            if valid(tau - LAG_EXP) and tau - LAG_EXP not in MASK_ON_TENSOR:
+            if valid(tau - LAG_EXP):
                 exponent(tau - LAG_EXP)
             if valid(tau - LAG_MX) and not valid(tau + 2):
                 weighted_sum(tau - LAG_MX)
@@ -401,8 +384,6 @@ def tile_single_head_split_window_attention_t_kernel(
                 scores_half(tau + 2, 1)
             if valid(tau - LAG_QUANTISE):
                 quantise_e(tau - LAG_QUANTISE)
-            if tau - LAG_JOIN in MASK_ON_TENSOR:
-                join_sums(tau - LAG_JOIN)
             if valid(tau - LAG_RECIPROCAL) and (tau - LAG_RECIPROCAL) % GROUP == 0:
                 reciprocal((tau - LAG_RECIPROCAL) // GROUP)
             if win < NWIN and blk == 3:
@@ -411,8 +392,6 @@ def tile_single_head_split_window_attention_t_kernel(
                 row_max(tau)
             if valid(tau - LAG_REGROUP):
                 regroup(tau - LAG_REGROUP)
-            if tau in MASK_ON_TENSOR:
-                exponent(tau)
             if prepare and 0 <= part < 2:
                 keep_k(nxt, part, bank, False)
             if prepare and 2 <= part < 4:

@@ -70,16 +70,16 @@ def tile_single_head_split_window_attention_t_kernel(
         ident_f = res.tile([P, P], F32, name="ident_f")
         ident_b = res.tile([P, P], BF16, name="ident_b")
         ident_16 = res.tile([P, P], BF16, name="ident_16")
+        idle_src = res.tile([P, HALF], BF16, name="idle_src", align_bytes=64)
+        idle_codes = res.tile([P, P], U32, name="idle_codes", align_bytes=64)
+        idle_scales = res.tile([P, P], U8, name="idle_scales", align_bytes=64)
+        nc.gpsimd.memset(idle_src[:].bitcast(F32), 1.0)
+        nc.vector.quantize_mx(out=idle_codes[:].bitcast(FP8X4), scales=idle_scales[:], in_=idle_src[:])
         make_identity(nc, ident_f[:])
         make_identity(nc, ident_b[:])
         nc.gpsimd.tensor_scalar(
             out=ident_16[:], in0=ident_b[:], scalar1=1.0 / INV_SCALE, scalar2=0.0, op0=ALU.mult, op1=ALU.add
         )
-
-        warm_in = res.tile([P, 1], F32, name="warm_in")
-        warm_out = res.tile([P, 1], F32, name="warm_out")
-        nc.vector.memset(warm_in[:], 0.0)
-        nc.scalar.activation(out=warm_out[:], in_=warm_in[:], func=ACT.Exp)
 
         q_sb = [res.tile([P, NBLK, C], BF16, name="q_sb%d" % i) for i in range(NWIN)]
         k_sb = [res.tile([P, NBLK, C], BF16, name="k_sb%d" % i) for i in range(NWIN)]
@@ -91,10 +91,10 @@ def tile_single_head_split_window_attention_t_kernel(
         mask_sb = [res.tile([P, L], BF16, name="mask%d" % i) for i in range(NT)]
 
 
-        def load_slabs(dst, src, win, lo, hi):
+        def load_slabs(dst, src, win, lo, hi, queue=nc.sync):
             for slab in range(lo, hi):
                 yq, xq = image_slab(win, slab)
-                nc.sync.dma_start(
+                queue.dma_start(
                     out=dst[win][:, 2 * slab : 2 * slab + 2, :].rearrange("p j c -> p (j c)"), in_=src[0, yq, xq]
                 )
 
@@ -104,9 +104,16 @@ def tile_single_head_split_window_attention_t_kernel(
             g, u = divmod(slab, 2)
             nc.sync.dma_start(out=mask_sb[t][:, lo:hi], in_=m_blk[win, g, u, e, :, :, lo:hi])
 
-        load_slabs(k_sb, k_slab, 0, 0, 2)
+        load_slabs(k_sb, k_slab, 0, 0, 1)
+        load_slabs(k_sb, k_slab, 0, 1, 2, nc.scalar)
         load_slabs(q_sb, q_slab, 0, 0, 1)
-        load_slabs(k_sb, k_slab, 0, 2, 4)
+        load_slabs(k_sb, k_slab, 0, 2, 3, nc.scalar)
+        load_slabs(k_sb, k_slab, 0, 3, 4)
+        warm_in = res.tile([P, 1], F32, name="warm_in")
+        warm_out = res.tile([P, 1], F32, name="warm_out")
+        nc.vector.memset(warm_in[:], 0.0)
+        nc.scalar.activation(out=warm_out[:], in_=warm_in[:], func=ACT.Exp)
+
         load_mask(0, 0, HALF)
         load_mask(0, HALF, L)
         load_mask(1, 0, L)
@@ -148,13 +155,19 @@ def tile_single_head_split_window_attention_t_kernel(
             else:
                 nc.scalar.copy(out=dst_ap, in_=bank[:, 0:n, :])
 
-        def keep_k(win, yh, bank, on_vector):
-            dst_ap = k_t[win][:, yh, :].rearrange("p (rr u x8 e) -> p u rr x8 e", rr=16, u=2, x8=8, e=2)
-            src_ap = bank[:].rearrange("p (u e) (rr x8) -> p u rr x8 e", u=2, e=2, rr=16, x8=8)
+        def keep_k(win, yh, bank):
+            nc.scalar.copy(
+                out=k_t[win][:, yh, :].rearrange("p (rr u x8 e) -> p u rr x8 e", rr=16, u=2, x8=8, e=2),
+                in_=bank[:].rearrange("p (u e) (rr x8) -> p u rr x8 e", u=2, e=2, rr=16, x8=8),
+            )
+
+        def keep_k_slab(win, yh, u, bank, on_vector):
+            dst = k_t[win][:, yh, :].rearrange("p (rr u x8 e) -> p u rr x8 e", rr=16, u=2, x8=8, e=2)[:, u]
+            src = bank[:, 0:2, :].rearrange("p e (rr x8) -> p rr x8 e", rr=16, x8=8)
             if on_vector:
-                nc.vector.tensor_copy(out=dst_ap, in_=src_ap)
+                nc.vector.tensor_copy(out=dst, in_=src)
             else:
-                nc.scalar.copy(out=dst_ap, in_=src_ap)
+                nc.scalar.copy(out=dst, in_=src)
 
         v_grouped = {}
 
@@ -227,36 +240,37 @@ def tile_single_head_split_window_attention_t_kernel(
             scores_half(t, 1)
 
         def add_mask(t):
-            x = work.tile([P, L], F32, name="x", tag="x")
-            x_tiles[t] = x
+            x_tiles[t] = work.tile([P, L], F32, name="x", tag="x")
             if t in MASK_ON_TENSOR:
-                halves[t] = stat.tile([P, 2], F32, name="half_min", tag="half_min")
+                halves[t] = stat.tile([P, 1], F32, name="half_min", tag="half_min")
+                bring_out(t, 0, None, halves[t])
+                return
             for half in range(2):
                 cols = slice(HALF * half, HALF * half + HALF)
-                if t in MASK_ON_TENSOR:
-                    nc.vector.tensor_scalar(
-                        out=x[:, cols],
-                        in0=s_tiles[(t, half)][:],
-                        scalar1=-INV_SCALE,
-                        scalar2=None,
-                        op0=ALU.mult,
-                        op1=ALU.min,
-                        accum_out=halves[t][:, half : half + 1],
-                    )
-                else:
-                    nc.vector.scalar_tensor_tensor(
-                        out=x[:, cols],
-                        in0=s_tiles[(t, half)][:],
-                        scalar=INV_SCALE,
-                        in1=mask_sb[t][:, cols],
-                        op0=ALU.mult,
-                        op1=ALU.add,
-                    )
+                nc.vector.scalar_tensor_tensor(
+                    out=x_tiles[t][:, cols],
+                    in0=s_tiles[(t, half)][:],
+                    scalar=INV_SCALE,
+                    in1=mask_sb[t][:, cols],
+                    op0=ALU.mult,
+                    op1=ALU.add,
+                )
+
+        def bring_out(t, half, seed, least):
+            nc.vector.tensor_scalar(
+                out=x_tiles[t][:, HALF * half : HALF * half + HALF],
+                in0=s_tiles[(t, half)][:],
+                scalar1=-INV_SCALE,
+                scalar2=seed,
+                op0=ALU.mult,
+                op1=ALU.min,
+                accum_out=least[:],
+            )
 
         def row_max(t):
             negs[t] = stat.tile([P, 1], F32, name="neg_max", tag="neg_max")
             if t in MASK_ON_TENSOR:
-                nc.vector.tensor_reduce(out=negs[t][:], in_=halves[t][:], axis=AX.X, op=ALU.min)
+                bring_out(t, 1, halves[t][:], negs[t])
             else:
                 nc.vector.tensor_reduce(out=negs[t][:], in_=x_tiles[t][:], axis=AX.X, op=ALU.max, negate=True)
 
@@ -291,7 +305,7 @@ def tile_single_head_split_window_attention_t_kernel(
             g_tiles[t] = work.tile([P, 2, P, 4], BF16, name="grouped", tag="grouped", bufs=4, align_bytes=64)
             src = et_tiles[t][:].rearrange("p g u q -> p g q u")
             dst = g_tiles[t][:].rearrange("p g q j -> p g (q j)").bitcast(F32).rearrange("p g (q u) -> p g q u", u=2)
-            if t == NT - 3:
+            if t in (NT - 3, NT - 2):
                 nc.vector.tensor_copy(out=dst, in_=src)
             else:
                 nc.scalar.copy(out=dst, in_=src)
@@ -337,17 +351,32 @@ def tile_single_head_split_window_attention_t_kernel(
         def valid(t):
             return 0 <= t < NT
 
-        bank = transpose_blocks(k_sb, 0, [0, 1, 2, 3], ps_m, "misc")
-        keep_k(0, 0, bank, True)
-        bank = transpose_blocks(q_sb, 0, [0, 1], ps_m, "misc")
-        keep_q(0, [0, 1], bank, False)
-        bank = transpose_blocks(k_sb, 0, [4, 5, 6, 7], ps_e, "e_t")
-        keep_k(0, 1, bank, False)
+        idle_ps = ps_s.tile([P, HALF], F32, name="s_ps0", tag="s_ps0")
+        for idle in range(16):
+            nc.tensor.matmul_mx(
+                out=idle_ps[:, 0:P],
+                lhsT=idle_codes[:].bitcast(FP8X4),
+                lhsT_scale=idle_scales[:],
+                rhs=idle_codes[:].bitcast(FP8X4),
+                rhs_scale=idle_scales[:],
+                start=True,
+                stop=True,
+            )
+        bank = transpose_blocks(k_sb, 0, [0, 1], ps_m, "misc")
+        keep_k_slab(0, 0, 0, bank, True)
+        bank = transpose_blocks(k_sb, 0, [2, 3], ps_m, "misc")
+        keep_k_slab(0, 0, 1, bank, False)
+        bank = transpose_blocks(q_sb, 0, [0, 1], ps_e, "e_t")
+        keep_q(0, [0, 1], bank, True)
+        bank = transpose_blocks(k_sb, 0, [4, 5], ps_e, "e_t")
+        keep_k_slab(0, 1, 0, bank, False)
+        bank = transpose_blocks(k_sb, 0, [6, 7], ps_m, "misc")
+        keep_k_slab(0, 1, 1, bank, True)
         scores(0)
         scores(1)
-        bank = transpose_blocks(q_sb, 0, [2, 3], ps_e, "e_t")
+        bank = transpose_blocks(q_sb, 0, [2, 3], ps_m, "misc")
         keep_q(0, [2, 3], bank, False)
-        bank = transpose_blocks(q_sb, 0, [4, 5, 6, 7], ps_m, "misc")
+        bank = transpose_blocks(q_sb, 0, [4, 5, 6, 7], ps_e, "e_t")
         keep_q(0, [4, 5, 6, 7], bank, False)
         group_v(0)
 
@@ -358,7 +387,7 @@ def tile_single_head_split_window_attention_t_kernel(
             part = blk - 3
             group = [4 * (part % 2) + i for i in range(4)]
             last = tau - LAG_FINISH
-            last_on_vector = last >= NT - 5
+            last_on_vector = last == NT - 1
 
             load_round(ROUNDS_AHEAD + tau)
             if prepare and blk == 7:
@@ -393,6 +422,6 @@ def tile_single_head_split_window_attention_t_kernel(
             if valid(tau - LAG_REGROUP):
                 regroup(tau - LAG_REGROUP)
             if prepare and 0 <= part < 2:
-                keep_k(nxt, part, bank, False)
+                keep_k(nxt, part, bank)
             if prepare and 2 <= part < 4:
                 keep_q(nxt, group, bank, False)

@@ -174,16 +174,9 @@ def tile_single_head_split_window_attention_t_kernel(
         def group_v(win):
             vg = work.tile([P, 2, C, 4], BF16, name="vg", tag="vg", bufs=2, align_bytes=64)
             src = v_sb[win][:].rearrange("p (g j) c -> p g c j", g=2, j=4)
-            for g in range(2):
-                for lo in range(0, C, P):
-                    nc.gpsimd.tensor_scalar(
-                        out=vg[:, g, lo : lo + P, :],
-                        in0=src[:, g, lo : lo + P, :],
-                        scalar1=1.0,
-                        scalar2=0.0,
-                        op0=ALU.mult,
-                        op1=ALU.add,
-                    )
+            nc.gpsimd.tensor_scalar(
+                out=vg[:], in0=src, scalar1=1.0, scalar2=0.0, op0=ALU.mult, op1=ALU.add
+            )
             v_grouped[win] = vg
 
         def quantise_v(win):
@@ -352,7 +345,7 @@ def tile_single_head_split_window_attention_t_kernel(
             return 0 <= t < NT
 
         idle_ps = ps_s.tile([P, HALF], F32, name="s_ps0", tag="s_ps0")
-        for idle in range(16):
+        for idle in range(11):
             nc.tensor.matmul_mx(
                 out=idle_ps[:, 0:P],
                 lhsT=idle_codes[:].bitcast(FP8X4),

@@ -112,6 +112,8 @@ def tile_single_head_split_window_attention_t_kernel(
         warm_in = res.tile([P, 1], F32, name="warm_in")
         warm_out = res.tile([P, 1], F32, name="warm_out")
         nc.vector.memset(warm_in[:], 0.0)
+        ones = res.tile([P, 1], F32, name="ones")
+        nc.vector.memset(ones[:], 1.0)
         nc.scalar.activation(out=warm_out[:], in_=warm_in[:], func=ACT.Exp)
 
         load_mask(0, 0, HALF)
@@ -171,13 +173,23 @@ def tile_single_head_split_window_attention_t_kernel(
 
         v_grouped = {}
 
-        def group_v(win):
-            vg = work.tile([P, 2, C, 4], BF16, name="vg", tag="vg", bufs=2, align_bytes=64)
-            src = v_sb[win][:].rearrange("p (g j) c -> p g c j", g=2, j=4)
+        def group_v(win, g):
+            if g == 0:
+                v_grouped[win] = work.tile([P, 2, C, 4], BF16, name="vg", tag="vg", bufs=2, align_bytes=64)
+            one = stat.tile([P, 1], F32, name="one", tag="one")
+            nc.scalar.copy(out=one[:], in_=ones[:])
             nc.gpsimd.tensor_scalar(
-                out=vg[:], in0=src, scalar1=1.0, scalar2=0.0, op0=ALU.mult, op1=ALU.add
+                out=v_grouped[win][:, g],
+                in0=v_sb[win][:].rearrange("p (g j) c -> p g c j", g=2, j=4)[:, g],
+                scalar1=one[:, 0:1],
+                scalar2=0.0,
+                op0=ALU.mult,
+                op1=ALU.add,
             )
-            v_grouped[win] = vg
+
+        v_rounds = []
+        for win in range(NWIN):
+            v_rounds += [t for t in range(NBLK * win + 1, NBLK * win + 4) if t not in MASK_ON_TENSOR][0:2]
 
         def quantise_v(win):
             nc.vector.quantize_mx(
@@ -294,11 +306,16 @@ def tile_single_head_split_window_attention_t_kernel(
             recips[grp] = stat.tile([P, GROUP], F32, name="recip", tag="recip")
             nc.vector.reciprocal(out=recips[grp][:], in_=sum_groups[grp][:])
 
-        def regroup(t):
+        def regroup(t, on_vector):
             g_tiles[t] = work.tile([P, 2, P, 4], BF16, name="grouped", tag="grouped", bufs=4, align_bytes=64)
-            src = et_tiles[t][:].rearrange("p g u q -> p g q u")
-            dst = g_tiles[t][:].rearrange("p g q j -> p g (q j)").bitcast(F32).rearrange("p g (q u) -> p g q u", u=2)
-            if t in (NT - 3, NT - 2):
+            move_words(
+                g_tiles[t][:].rearrange("p g q j -> p g (q j)").bitcast(F32).rearrange("p g (q u) -> p g q u", u=2),
+                et_tiles[t][:].rearrange("p g u q -> p g q u"),
+                on_vector,
+            )
+
+        def move_words(dst, src, on_vector):
+            if on_vector:
                 nc.vector.tensor_copy(out=dst, in_=src)
             else:
                 nc.scalar.copy(out=dst, in_=src)
@@ -313,33 +330,91 @@ def tile_single_head_split_window_attention_t_kernel(
                 in_=g_tiles[t][:].rearrange("p g q j -> p (g q j)"),
             )
 
-        def weighted_sum(t):
+        def weighted_half(t, g, o_ps):
             win = t // NBLK
             codes, scales = c_tiles[t]
-            o_tiles[t] = ps_m.tile([P, C], F32, name="o_ps", tag="misc")
-            for g in range(2):
-                nc.tensor.matmul_mx(
-                    out=o_tiles[t][:],
-                    lhsT=codes[:, P * g : P * g + P].bitcast(FP8X4),
-                    lhsT_scale=scales[:, P * g : P * g + P],
-                    rhs=v_codes[win][:, C * g : C * g + C].bitcast(FP8X4),
-                    rhs_scale=v_scales[win][:, C * g : C * g + C],
-                    start=(g == 0),
-                    stop=(g == 1),
-                )
+            nc.tensor.matmul_mx(
+                out=o_ps[:, 0:C],
+                lhsT=codes[:, P * g : P * g + P].bitcast(FP8X4),
+                lhsT_scale=scales[:, P * g : P * g + P],
+                rhs=v_codes[win][:, C * g : C * g + C].bitcast(FP8X4),
+                rhs_scale=v_scales[win][:, C * g : C * g + C],
+                start=(g == 0),
+                stop=(g == 1),
+            )
 
-        def finish(t, on_vector):
+        def weighted_sum(t):
+            o_tiles[t] = ps_m.tile([P, C], F32, name="o_ps", tag="misc")
+            weighted_half(t, 0, o_tiles[t])
+            weighted_half(t, 1, o_tiles[t])
+
+        def finish(t, o_ps, on_vector):
             win, blk = divmod(t, NBLK)
-            o_sb = work.tile([P, C], F32, name="o_sb", tag="o_sb", bufs=6)
+            o_sb = work.tile([P, C], F32, name="o_sb", tag="o_sb", bufs=10)
             recip = recips[t // GROUP][:, t % GROUP : t % GROUP + 1]
             if on_vector:
                 nc.vector.tensor_scalar(
-                    out=o_sb[:], in0=o_tiles[t][:], scalar1=recip, scalar2=None, op0=ALU.mult
+                    out=o_sb[:], in0=o_ps[:, 0:C], scalar1=recip, scalar2=None, op0=ALU.mult
                 )
             else:
-                nc.scalar.activation(out=o_sb[:], in_=o_tiles[t][:], func=ACT.Copy, scale=recip)
+                nc.scalar.activation(out=o_sb[:], in_=o_ps[:, 0:C], func=ACT.Copy, scale=recip)
             yq, xq = image_slab(win, blk // 2)
             nc.sync.dma_start(out=o_blk[0, yq, xq, blk % 2], in_=o_sb[:])
+
+
+        def exponent_half(t, g):
+            if g == 0:
+                e_tiles[t] = work.tile([P, 2, 2, 16, 16], BF16, name="e_sb", tag="e_sb")
+                halves[t] = stat.tile([P, 2], F32, name="half_sum", tag="half_sum")
+            nc.scalar.activation(
+                out=e_tiles[t][:, g].rearrange("p u r w -> p r u w"),
+                in_=x_tiles[t][:, HALF * g : HALF * g + HALF].rearrange("p (r u w) -> p r u w", r=16, u=2, w=16),
+                func=ACT.Exp,
+                bias=negs[t][:, 0:1],
+                scale=1.0,
+                accum_out=halves[t][:, g : g + 1],
+            )
+
+        def join_sums(t):
+            nc.vector.tensor_reduce(out=sum_column(t), in_=halves[t][:], axis=AX.X, op=ALU.add)
+
+        def transpose_half(t, g):
+            et_tiles[(t, g)] = spare_bank(g)
+            for u in range(2):
+                nc.tensor.transpose(
+                    out=et_tiles[(t, g)][:, P * u : P * u + P],
+                    in_=e_tiles[t][:, g, u].rearrange("p r w -> p (r w)").bitcast(F32),
+                    identity=ident_f[:],
+                )
+
+        def regroup_half(t, g, on_vector):
+            if g == 0:
+                g_tiles[t] = work.tile([P, 2, P, 4], BF16, name="grouped", tag="grouped", bufs=4, align_bytes=64)
+            move_words(
+                g_tiles[t][:, g].rearrange("p q j -> p (q j)").bitcast(F32).rearrange("p (q u) -> p q u", u=2),
+                et_tiles[(t, g)][:, 0 : 2 * P].rearrange("p (u q) -> p q u", u=2),
+                on_vector,
+            )
+
+        def quantise_half(t, g):
+            if g == 0:
+                codes = work.tile([P, 2 * P], U32, name="codes", tag="codes", align_bytes=64)
+                scales = work.tile([P, 2 * P], U8, name="scales", tag="scales", align_bytes=64)
+                c_tiles[t] = (codes, scales)
+            codes, scales = c_tiles[t]
+            nc.vector.quantize_mx(
+                out=codes[:, P * g : P * g + P].bitcast(FP8X4),
+                scales=scales[:, P * g : P * g + P],
+                in_=g_tiles[t][:, g].rearrange("p q j -> p (q j)"),
+            )
+
+        def spare_bank(h):
+            return ps_s.tile([P, HALF], F32, name="s_ps%d" % h, tag="s_ps%d" % h)
+
+        def weighted_in(t, bank):
+            o_tiles[t] = bank
+            weighted_half(t, 0, bank)
+            weighted_half(t, 1, bank)
 
         def valid(t):
             return 0 <= t < NT
@@ -359,36 +434,36 @@ def tile_single_head_split_window_attention_t_kernel(
         keep_k_slab(0, 0, 0, bank, True)
         bank = transpose_blocks(k_sb, 0, [2, 3], ps_m, "misc")
         keep_k_slab(0, 0, 1, bank, False)
-        bank = transpose_blocks(q_sb, 0, [0, 1], ps_e, "e_t")
-        keep_q(0, [0, 1], bank, True)
+        bank = transpose_blocks(q_sb, 0, [0], ps_e, "e_t")
+        keep_q(0, [0], bank, True)
         bank = transpose_blocks(k_sb, 0, [4, 5], ps_e, "e_t")
         keep_k_slab(0, 1, 0, bank, False)
         bank = transpose_blocks(k_sb, 0, [6, 7], ps_m, "misc")
         keep_k_slab(0, 1, 1, bank, True)
+        bank = transpose_blocks(q_sb, 0, [1], ps_m, "misc")
+        keep_q(0, [1], bank, False)
         scores(0)
         scores(1)
         bank = transpose_blocks(q_sb, 0, [2, 3], ps_m, "misc")
         keep_q(0, [2, 3], bank, False)
         bank = transpose_blocks(q_sb, 0, [4, 5, 6, 7], ps_e, "e_t")
         keep_q(0, [4, 5, 6, 7], bank, False)
-        group_v(0)
 
-        for tau in range(NT + LAG_FINISH):
+        for tau in range(NT):
             win, blk = divmod(tau, NBLK)
             nxt = win + 1
             prepare = nxt < NWIN
             part = blk - 3
             group = [4 * (part % 2) + i for i in range(4)]
             last = tau - LAG_FINISH
-            last_on_vector = last == NT - 1
 
             load_round(ROUNDS_AHEAD + tau)
-            if prepare and blk == 7:
-                group_v(nxt)
-            if valid(last) and not last_on_vector:
-                finish(last, False)
+            if valid(last):
+                finish(last, o_tiles[last], False)
             if valid(tau - LAG_EXP):
                 exponent(tau - LAG_EXP)
+            if tau in v_rounds:
+                group_v(win, v_rounds.index(tau) % 2)
             if valid(tau - LAG_MX) and not valid(tau + 2):
                 weighted_sum(tau - LAG_MX)
             if valid(tau - LAG_TRANSPOSE):
@@ -397,8 +472,6 @@ def tile_single_head_split_window_attention_t_kernel(
                 bank = transpose_blocks(k_sb if part < 2 else q_sb, nxt, group, ps_m, "misc")
             if valid(tau):
                 add_mask(tau)
-            if valid(last) and last_on_vector:
-                finish(last, True)
             if valid(tau + 2):
                 scores_half(tau + 2, 0)
                 if valid(tau - LAG_MX):
@@ -408,13 +481,46 @@ def tile_single_head_split_window_attention_t_kernel(
                 quantise_e(tau - LAG_QUANTISE)
             if valid(tau - LAG_RECIPROCAL) and (tau - LAG_RECIPROCAL) % GROUP == 0:
                 reciprocal((tau - LAG_RECIPROCAL) // GROUP)
-            if win < NWIN and blk == 3:
+            if blk == 5:
                 quantise_v(win)
             if valid(tau):
                 row_max(tau)
             if valid(tau - LAG_REGROUP):
-                regroup(tau - LAG_REGROUP)
+                regroup(tau - LAG_REGROUP, False)
             if prepare and 0 <= part < 2:
                 keep_k(nxt, part, bank)
             if prepare and 2 <= part < 4:
                 keep_q(nxt, group, bank, False)
+
+        finish(25, o_tiles[25], False)
+        exponent_half(31, 0)
+        exponent_half(31, 1)
+        weighted_sum(26)
+        transpose_e(30)
+        quantise_e(27)
+        regroup(29, True)
+        weighted_sum(27)
+        transpose_half(31, 0)
+        quantise_e(28)
+        finish(26, o_tiles[26], False)
+        regroup(30, True)
+        regroup_half(31, 0, False)
+        transpose_half(31, 1)
+        weighted_in(28, spare_bank(0))
+        finish(27, o_tiles[27], False)
+        regroup_half(31, 1, False)
+        quantise_e(29)
+        join_sums(31)
+        weighted_in(29, spare_bank(1))
+        quantise_half(31, 0)
+        reciprocal(7)
+        quantise_e(30)
+        o_tiles[31] = ps_e.tile([P, HALF], F32, name="e_t", tag="e_t")
+        weighted_half(31, 0, o_tiles[31])
+        quantise_half(31, 1)
+        weighted_in(30, ps_e.tile([P, HALF], F32, name="e_t", tag="e_t"))
+        weighted_half(31, 1, o_tiles[31])
+        finish(28, o_tiles[28], False)
+        finish(29, o_tiles[29], False)
+        finish(30, o_tiles[30], False)
+        finish(31, o_tiles[31], True)

@@ -149,6 +149,19 @@ def tile_single_head_split_window_attention_t_kernel(
                 )
             return bank
 
+        def idle_passes(count):
+            bank = ps_s.tile([P, HALF], F32, name="s_ps0", tag="s_ps0")
+            for i in range(count):
+                nc.tensor.matmul_mx(
+                    out=bank[:, 0:P],
+                    lhsT=idle_codes[:].bitcast(FP8X4),
+                    lhsT_scale=idle_scales[:],
+                    rhs=idle_codes[:].bitcast(FP8X4),
+                    rhs_scale=idle_scales[:],
+                    start=True,
+                    stop=True,
+                )
+
         def keep_q(win, group, bank, on_vector):
             n = len(group)
             dst_ap = q_t[win][:, group[0] : group[0] + n, :]
@@ -244,22 +257,23 @@ def tile_single_head_split_window_attention_t_kernel(
             scores_half(t, 0)
             scores_half(t, 1)
 
-        def add_mask(t):
-            x_tiles[t] = work.tile([P, L], F32, name="x", tag="x")
+        def add_mask(t, half):
+            if half == 0:
+                x_tiles[t] = work.tile([P, L], F32, name="x", tag="x")
             if t in MASK_ON_TENSOR:
-                halves[t] = stat.tile([P, 1], F32, name="half_min", tag="half_min")
-                bring_out(t, 0, None, halves[t])
+                if half == 0:
+                    halves[t] = stat.tile([P, 1], F32, name="half_min", tag="half_min")
+                    bring_out(t, 0, None, halves[t])
                 return
-            for half in range(2):
-                cols = slice(HALF * half, HALF * half + HALF)
-                nc.vector.scalar_tensor_tensor(
-                    out=x_tiles[t][:, cols],
-                    in0=s_tiles[(t, half)][:],
-                    scalar=INV_SCALE,
-                    in1=mask_sb[t][:, cols],
-                    op0=ALU.mult,
-                    op1=ALU.add,
-                )
+            cols = slice(HALF * half, HALF * half + HALF)
+            nc.vector.scalar_tensor_tensor(
+                out=x_tiles[t][:, cols],
+                in0=s_tiles[(t, half)][:],
+                scalar=INV_SCALE,
+                in1=mask_sb[t][:, cols],
+                op0=ALU.mult,
+                op1=ALU.add,
+            )
 
         def bring_out(t, half, seed, least):
             nc.vector.tensor_scalar(
@@ -321,8 +335,8 @@ def tile_single_head_split_window_attention_t_kernel(
                 nc.scalar.copy(out=dst, in_=src)
 
         def quantise_e(t):
-            codes = work.tile([P, 2 * P], U32, name="codes", tag="codes", align_bytes=64)
-            scales = work.tile([P, 2 * P], U8, name="scales", tag="scales", align_bytes=64)
+            codes = work.tile([P, 2 * P], U32, name="codes", tag="codes", bufs=5, align_bytes=64)
+            scales = work.tile([P, 2 * P], U8, name="scales", tag="scales", bufs=5, align_bytes=64)
             c_tiles[t] = (codes, scales)
             nc.vector.quantize_mx(
                 out=codes[:].bitcast(FP8X4),
@@ -398,8 +412,8 @@ def tile_single_head_split_window_attention_t_kernel(
 
         def quantise_half(t, g):
             if g == 0:
-                codes = work.tile([P, 2 * P], U32, name="codes", tag="codes", align_bytes=64)
-                scales = work.tile([P, 2 * P], U8, name="scales", tag="scales", align_bytes=64)
+                codes = work.tile([P, 2 * P], U32, name="codes", tag="codes", bufs=5, align_bytes=64)
+                scales = work.tile([P, 2 * P], U8, name="scales", tag="scales", bufs=5, align_bytes=64)
                 c_tiles[t] = (codes, scales)
             codes, scales = c_tiles[t]
             nc.vector.quantize_mx(
@@ -419,17 +433,7 @@ def tile_single_head_split_window_attention_t_kernel(
         def valid(t):
             return 0 <= t < NT
 
-        idle_ps = ps_s.tile([P, HALF], F32, name="s_ps0", tag="s_ps0")
-        for idle in range(11):
-            nc.tensor.matmul_mx(
-                out=idle_ps[:, 0:P],
-                lhsT=idle_codes[:].bitcast(FP8X4),
-                lhsT_scale=idle_scales[:],
-                rhs=idle_codes[:].bitcast(FP8X4),
-                rhs_scale=idle_scales[:],
-                start=True,
-                stop=True,
-            )
+        idle_passes(11)
         bank = transpose_blocks(k_sb, 0, [0, 1], ps_m, "misc")
         keep_k_slab(0, 0, 0, bank, True)
         bank = transpose_blocks(k_sb, 0, [2, 3], ps_m, "misc")
@@ -440,7 +444,7 @@ def tile_single_head_split_window_attention_t_kernel(
         keep_k_slab(0, 1, 0, bank, False)
         bank = transpose_blocks(k_sb, 0, [6, 7], ps_m, "misc")
         keep_k_slab(0, 1, 1, bank, True)
-        bank = transpose_blocks(q_sb, 0, [1], ps_m, "misc")
+        bank = transpose_blocks(q_sb, 0, [1], ps_s, "s_ps1")
         keep_q(0, [1], bank, False)
         scores(0)
         scores(1)
@@ -453,8 +457,7 @@ def tile_single_head_split_window_attention_t_kernel(
             win, blk = divmod(tau, NBLK)
             nxt = win + 1
             prepare = nxt < NWIN
-            part = blk - 3
-            group = [4 * (part % 2) + i for i in range(4)]
+            part = blk - 2
             last = tau - LAG_FINISH
 
             load_round(ROUNDS_AHEAD + tau)
@@ -464,33 +467,37 @@ def tile_single_head_split_window_attention_t_kernel(
                 exponent(tau - LAG_EXP)
             if tau in v_rounds:
                 group_v(win, v_rounds.index(tau) % 2)
-            if valid(tau - LAG_MX) and not valid(tau + 2):
-                weighted_sum(tau - LAG_MX)
+            if prepare and 1 <= part < 3:
+                keep_k(nxt, part - 1, bank)
+            if prepare and 3 <= part < 5:
+                keep_q(nxt, group, bank, False)
             if valid(tau - LAG_TRANSPOSE):
                 transpose_e(tau - LAG_TRANSPOSE)
-            if prepare and 0 <= part < 4:
-                bank = transpose_blocks(k_sb if part < 2 else q_sb, nxt, group, ps_m, "misc")
-            if valid(tau):
-                add_mask(tau)
+            if not valid(tau + 2):
+                idle_passes(14)
+                weighted_sum(tau - LAG_MX)
+            if tau == 0 or tau > LAG_QUANTISE:
+                add_mask(tau, 0)
+            add_mask(tau, 1)
             if valid(tau + 2):
                 scores_half(tau + 2, 0)
                 if valid(tau - LAG_MX):
                     weighted_sum(tau - LAG_MX)
                 scores_half(tau + 2, 1)
+            if prepare and 0 <= part < 4:
+                group = [4 * (part % 2) + i for i in range(4)]
+                bank = transpose_blocks(k_sb if part < 2 else q_sb, nxt, group, ps_m, "misc")
             if valid(tau - LAG_QUANTISE):
                 quantise_e(tau - LAG_QUANTISE)
             if valid(tau - LAG_RECIPROCAL) and (tau - LAG_RECIPROCAL) % GROUP == 0:
                 reciprocal((tau - LAG_RECIPROCAL) // GROUP)
             if blk == 5:
                 quantise_v(win)
-            if valid(tau):
-                row_max(tau)
+            if tau < LAG_QUANTISE:
+                add_mask(tau + 1, 0)
+            row_max(tau)
             if valid(tau - LAG_REGROUP):
                 regroup(tau - LAG_REGROUP, False)
-            if prepare and 0 <= part < 2:
-                keep_k(nxt, part, bank)
-            if prepare and 2 <= part < 4:
-                keep_q(nxt, group, bank, False)
 
         finish(25, o_tiles[25], False)
         exponent_half(31, 0)
@@ -502,25 +509,25 @@ def tile_single_head_split_window_attention_t_kernel(
         weighted_sum(27)
         transpose_half(31, 0)
         quantise_e(28)
+        regroup_half(31, 0, False)
         finish(26, o_tiles[26], False)
         regroup(30, True)
-        regroup_half(31, 0, False)
         transpose_half(31, 1)
         weighted_in(28, spare_bank(0))
-        finish(27, o_tiles[27], False)
         regroup_half(31, 1, False)
         quantise_e(29)
         join_sums(31)
         weighted_in(29, spare_bank(1))
         quantise_half(31, 0)
         reciprocal(7)
+        finish(27, o_tiles[27], False)
         quantise_e(30)
         o_tiles[31] = ps_e.tile([P, HALF], F32, name="e_t", tag="e_t")
         weighted_half(31, 0, o_tiles[31])
         quantise_half(31, 1)
         weighted_in(30, ps_e.tile([P, HALF], F32, name="e_t", tag="e_t"))
         weighted_half(31, 1, o_tiles[31])
-        finish(28, o_tiles[28], False)
+        finish(28, o_tiles[28], True)
         finish(29, o_tiles[29], False)
         finish(30, o_tiles[30], False)
         finish(31, o_tiles[31], True)

from contextlib import ExitStack

import concourse.mybir as mybir
from concourse.masks import make_identity

FLOPS = 2 * 2 * 4 * 1024 * 1024 * 256

F32 = mybir.dt.float32
BF16 = mybir.dt.bfloat16
U32 = mybir.dt.uint32
U8 = mybir.dt.uint8
FP8X4 = mybir.dt.float8_e4m3fn_x4
ALU = mybir.AluOpType
ACT = mybir.ActivationFunctionType
AX = mybir.AxisListType

P = 128
C = 256
NWIN = 4
NBLK = 8
L = 1024
HALF = 512
NT = NWIN * NBLK
INV_SCALE = 0.0625

MASK_ON_TENSOR = tuple(range(2, NT, 5))

LAG_EXP = 1
LAG_TRANSPOSE = 2
LAG_JOIN = 2
LAG_REGROUP = 3
LAG_QUANTISE = 5
LAG_MX = 6
LAG_FINISH = 7

GROUP = 4
LAG_RECIPROCAL = 6

FIRST_ROUND_MASK = 3
ROUNDS_AHEAD = 4


def image_slab(win, slab):
    wy, wx = divmod(win, 2)
    g, u = divmod(slab, 2)
    return (2 * wy + g + 1) % 4, (2 * wx + u + 1) % 4


def tile_single_head_split_window_attention_t_kernel(
    tc, q, k, v, attn_mask, num_splits, with_shift, h, w, out
):
    nc = tc.nc
    assert (num_splits, with_shift, h, w) == (2, 1, 64, 64)
    slabs = "o (yq rr xq x8 e) c -> o yq xq rr x8 (e c)"
    q_slab = q.rearrange(slabs, yq=4, rr=16, xq=4, x8=8, e=2)
    k_slab = k.rearrange(slabs, yq=4, rr=16, xq=4, x8=8, e=2)
    v_slab = v.rearrange(slabs, yq=4, rr=16, xq=4, x8=8, e=2)
    o_blk = out.rearrange("o (yq rr xq x8 e) c -> o yq xq e rr x8 c", yq=4, rr=16, xq=4, x8=8, e=2)
    m_blk = attn_mask.rearrange("j (g rr u x8 e) n -> j g u e rr x8 n", g=2, rr=16, u=2, x8=8, e=2)

    with ExitStack() as ctx:
        ctx.enter_context(tc.manual_schedule())
        res = ctx.enter_context(tc.tile_pool(name="res", bufs=1))
        work = ctx.enter_context(tc.tile_pool(name="work", bufs=3))
        stat = ctx.enter_context(tc.tile_pool(name="stat", bufs=10))
        ps_s = ctx.enter_context(tc.psum_pool(name="ps_s", bufs=2))
        ps_e = ctx.enter_context(tc.psum_pool(name="ps_e", bufs=2))
        ps_m = ctx.enter_context(tc.psum_pool(name="ps_m", bufs=2))

        ident_f = res.tile([P, P], F32, name="ident_f")
        ident_b = res.tile([P, P], BF16, name="ident_b")
        ident_16 = res.tile([P, P], BF16, name="ident_16")
        idle_src = res.tile([P, HALF], BF16, name="idle_src", align_bytes=64)
        idle_codes = res.tile([P, P], U32, name="idle_codes", align_bytes=64)
        idle_scales = res.tile([P, P], U8, name="idle_scales", align_bytes=64)
        nc.gpsimd.memset(idle_src[:].bitcast(F32), 1.0)
        nc.vector.quantize_mx(out=idle_codes[:].bitcast(FP8X4), scales=idle_scales[:], in_=idle_src[:])
        make_identity(nc, ident_f[:])
        make_identity(nc, ident_b[:])
        nc.gpsimd.tensor_scalar(
            out=ident_16[:], in0=ident_b[:], scalar1=1.0 / INV_SCALE, scalar2=0.0, op0=ALU.mult, op1=ALU.add
        )

        q_sb = [res.tile([P, NBLK, C], BF16, name="q_sb%d" % i) for i in range(NWIN)]
        k_sb = [res.tile([P, NBLK, C], BF16, name="k_sb%d" % i) for i in range(NWIN)]
        v_sb = [res.tile([P, NBLK, C], BF16, name="v_sb%d" % i) for i in range(NWIN)]
        q_t = [res.tile([P, NBLK, P], F32, name="q_t%d" % i) for i in range(NWIN)]
        k_t = [res.tile([P, 2, HALF], F32, name="k_t%d" % i) for i in range(NWIN)]
        v_codes = [res.tile([P, 2 * C], U32, name="v_codes%d" % i, align_bytes=64) for i in range(NWIN)]
        v_scales = [res.tile([P, 2 * C], U8, name="v_scales%d" % i, align_bytes=64) for i in range(NWIN)]
        mask_sb = [res.tile([P, L], BF16, name="mask%d" % i) for i in range(NT)]


        def load_slabs(dst, src, win, lo, hi, queue=nc.sync):
            for slab in range(lo, hi):
                yq, xq = image_slab(win, slab)
                queue.dma_start(
                    out=dst[win][:, 2 * slab : 2 * slab + 2, :].rearrange("p j c -> p (j c)"), in_=src[0, yq, xq]
                )

        def load_mask(t, lo, hi):
            win, blk = divmod(t, NBLK)
            slab, e = divmod(blk, 2)
            g, u = divmod(slab, 2)
            nc.sync.dma_start(out=mask_sb[t][:, lo:hi], in_=m_blk[win, g, u, e, :, :, lo:hi])

        load_slabs(k_sb, k_slab, 0, 0, 1)
        load_slabs(k_sb, k_slab, 0, 1, 2, nc.scalar)
        load_slabs(q_sb, q_slab, 0, 0, 1)
        load_slabs(k_sb, k_slab, 0, 2, 3, nc.scalar)
        load_slabs(k_sb, k_slab, 0, 3, 4)
        warm_in = res.tile([P, 1], F32, name="warm_in")
        warm_out = res.tile([P, 1], F32, name="warm_out")
        nc.vector.memset(warm_in[:], 0.0)
        ones = res.tile([P, 1], F32, name="ones")
        nc.vector.memset(ones[:], 1.0)
        nc.scalar.activation(out=warm_out[:], in_=warm_in[:], func=ACT.Exp)

        load_mask(0, 0, HALF)
        load_mask(0, HALF, L)
        load_mask(1, 0, L)
        load_slabs(q_sb, q_slab, 0, 1, 2)
        load_mask(2, 0, L)
        load_slabs(q_sb, q_slab, 0, 2, 4)
        load_slabs(v_sb, v_slab, 0, 0, 4)

        later = []
        for win in range(1, NWIN):
            for dst, src in ((k_sb, k_slab), (q_sb, q_slab), (v_sb, v_slab)):
                for lo in range(0, 4, 2):
                    later.append((dst, src, win, lo))

        def load_round(i):
            if FIRST_ROUND_MASK + i < NT:
                load_mask(FIRST_ROUND_MASK + i, 0, L)
            if i < len(later):
                dst, src, win, lo = later[i]
                load_slabs(dst, src, win, lo, lo + 2)

        for i in range(ROUNDS_AHEAD):
            load_round(i)


        def transpose_blocks(src, win, group, pool, tag):
            bank = pool.tile([P, 4, P], F32, name="bank_" + tag, tag=tag)
            for i, blk in enumerate(group):
                nc.tensor.transpose(
                    out=bank[:, i, :], in_=src[win][:, blk, :].bitcast(F32), identity=ident_f[:]
                )
            return bank

        def idle_passes(count):
            bank = ps_s.tile([P, HALF], F32, name="s_ps0", tag="s_ps0")
            for i in range(count):
                nc.tensor.matmul_mx(
                    out=bank[:, 0:P],
                    lhsT=idle_codes[:].bitcast(FP8X4),
                    lhsT_scale=idle_scales[:],
                    rhs=idle_codes[:].bitcast(FP8X4),
                    rhs_scale=idle_scales[:],
                    start=True,
                    stop=True,
                )

        def keep_q(win, group, bank, on_vector):
            n = len(group)
            dst_ap = q_t[win][:, group[0] : group[0] + n, :]
            if on_vector:
                nc.vector.tensor_copy(out=dst_ap, in_=bank[:, 0:n, :])
            else:
                nc.scalar.copy(out=dst_ap, in_=bank[:, 0:n, :])

        def keep_k(win, yh, bank):
            nc.scalar.copy(
                out=k_t[win][:, yh, :].rearrange("p (rr u x8 e) -> p u rr x8 e", rr=16, u=2, x8=8, e=2),
                in_=bank[:].rearrange("p (u e) (rr x8) -> p u rr x8 e", u=2, e=2, rr=16, x8=8),
            )

        def keep_k_slab(win, yh, u, bank, on_vector):
            dst = k_t[win][:, yh, :].rearrange("p (rr u x8 e) -> p u rr x8 e", rr=16, u=2, x8=8, e=2)[:, u]
            src = bank[:, 0:2, :].rearrange("p e (rr x8) -> p rr x8 e", rr=16, x8=8)
            if on_vector:
                nc.vector.tensor_copy(out=dst, in_=src)
            else:
                nc.scalar.copy(out=dst, in_=src)

        v_grouped = {}

        def group_v(win, g):
            if g == 0:
                v_grouped[win] = work.tile([P, 2, C, 4], BF16, name="vg", tag="vg", bufs=2, align_bytes=64)
            one = stat.tile([P, 1], F32, name="one", tag="one")
            nc.scalar.copy(out=one[:], in_=ones[:])
            nc.gpsimd.tensor_scalar(
                out=v_grouped[win][:, g],
                in0=v_sb[win][:].rearrange("p (g j) c -> p g c j", g=2, j=4)[:, g],
                scalar1=one[:, 0:1],
                scalar2=0.0,
                op0=ALU.mult,
                op1=ALU.add,
            )

        v_rounds = []
        for win in range(NWIN):
            v_rounds += [t for t in range(NBLK * win + 1, NBLK * win + 4) if t not in MASK_ON_TENSOR][0:2]

        def quantise_v(win):
            nc.vector.quantize_mx(
                out=v_codes[win][:].bitcast(FP8X4),
                scales=v_scales[win][:],
                in_=v_grouped[win][:].rearrange("p g c j -> p (g c j)"),
            )


        s_tiles = {}
        halves = {}
        x_tiles = {}
        e_tiles = {}
        et_tiles = {}
        g_tiles = {}
        c_tiles = {}
        o_tiles = {}
        negs = {}
        recips = {}
        sum_groups = {}

        def sum_column(t):
            grp, col = divmod(t, GROUP)
            if grp not in sum_groups:
                sum_groups[grp] = stat.tile([P, GROUP], F32, name="row_sums", tag="row_sums")
            return sum_groups[grp][:, col : col + 1]

        def scores_half(t, half):
            win, blk = divmod(t, NBLK)
            q_pair = q_t[win][:].bitcast(BF16).rearrange("p b (n e) -> p b n e", e=2)
            k_pair = k_t[win][:].bitcast(BF16).rearrange("p y (n e) -> p y n e", e=2)
            s_ps = ps_s.tile([P, HALF], F32, name="s_ps%d" % half, tag="s_ps%d" % half)
            s_tiles[(t, half)] = s_ps
            for e in range(2):
                nc.tensor.matmul(
                    out=s_ps[:],
                    lhsT=q_pair[:, blk, :, e],
                    rhs=k_pair[:, half, :, e],
                    start=(e == 0),
                    stop=(e == 1 and t not in MASK_ON_TENSOR),
                )
            if t in MASK_ON_TENSOR:
                nc.tensor.matmul(
                    out=s_ps[:],
                    lhsT=ident_16[:],
                    rhs=mask_sb[t][:, HALF * half : HALF * half + HALF],
                    start=False,
                    stop=True,
                )

        def scores(t):
            scores_half(t, 0)
            scores_half(t, 1)

        def add_mask(t, half):
            if half == 0:
                x_tiles[t] = work.tile([P, L], F32, name="x", tag="x")
            if t in MASK_ON_TENSOR:
                if half == 0:
                    halves[t] = stat.tile([P, 1], F32, name="half_min", tag="half_min")
                    bring_out(t, 0, None, halves[t])
                return
            cols = slice(HALF * half, HALF * half + HALF)
            nc.vector.scalar_tensor_tensor(
                out=x_tiles[t][:, cols],
                in0=s_tiles[(t, half)][:],
                scalar=INV_SCALE,
                in1=mask_sb[t][:, cols],
                op0=ALU.mult,
                op1=ALU.add,
            )

        def bring_out(t, half, seed, least):
            nc.vector.tensor_scalar(
                out=x_tiles[t][:, HALF * half : HALF * half + HALF],
                in0=s_tiles[(t, half)][:],
                scalar1=-INV_SCALE,
                scalar2=seed,
                op0=ALU.mult,
                op1=ALU.min,
                accum_out=least[:],
            )

        def row_max(t):
            negs[t] = stat.tile([P, 1], F32, name="neg_max", tag="neg_max")
            if t in MASK_ON_TENSOR:
                bring_out(t, 1, halves[t][:], negs[t])
            else:
                nc.vector.tensor_reduce(out=negs[t][:], in_=x_tiles[t][:], axis=AX.X, op=ALU.max, negate=True)

        def exponent(t):
            e_sb = work.tile([P, 2, 32, 16], BF16, name="e_sb", tag="e_sb")
            e_tiles[t] = e_sb
            nc.scalar.activation(
                out=e_sb[:].rearrange("p u r w -> p r u w"),
                in_=x_tiles[t][:].rearrange("p (r u w) -> p r u w", r=32, u=2, w=16),
                func=ACT.Exp,
                bias=negs[t][:, 0:1],
                scale=-1.0 if t in MASK_ON_TENSOR else 1.0,
                accum_out=sum_column(t),
            )

        def transpose_e(t):
            e_t = ps_e.tile([P, 2, 2, P], F32, name="e_t", tag="e_t")
            et_tiles[t] = e_t
            for g in range(2):
                for u in range(2):
                    nc.tensor.transpose(
                        out=e_t[:, g, u, :],
                        in_=e_tiles[t][:, u, 16 * g : 16 * g + 16, :].rearrange("p r w -> p (r w)").bitcast(F32),
                        identity=ident_f[:],
                    )

        def reciprocal(grp):
            recips[grp] = stat.tile([P, GROUP], F32, name="recip", tag="recip")
            nc.vector.reciprocal(out=recips[grp][:], in_=sum_groups[grp][:])

        def regroup(t, on_vector):
            g_tiles[t] = work.tile([P, 2, P, 4], BF16, name="grouped", tag="grouped", bufs=4, align_bytes=64)
            move_words(
                g_tiles[t][:].rearrange("p g q j -> p g (q j)").bitcast(F32).rearrange("p g (q u) -> p g q u", u=2),
                et_tiles[t][:].rearrange("p g u q -> p g q u"),
                on_vector,
            )

        def move_words(dst, src, on_vector):
            if on_vector:
                nc.vector.tensor_copy(out=dst, in_=src)
            else:
                nc.scalar.copy(out=dst, in_=src)

        def quantise_e(t):
            codes = work.tile([P, 2 * P], U32, name="codes", tag="codes", bufs=5, align_bytes=64)
            scales = work.tile([P, 2 * P], U8, name="scales", tag="scales", bufs=5, align_bytes=64)
            c_tiles[t] = (codes, scales)
            nc.vector.quantize_mx(
                out=codes[:].bitcast(FP8X4),
                scales=scales[:],
                in_=g_tiles[t][:].rearrange("p g q j -> p (g q j)"),
            )

        def weighted_half(t, g, o_ps):
            win = t // NBLK
            codes, scales = c_tiles[t]
            nc.tensor.matmul_mx(
                out=o_ps[:, 0:C],
                lhsT=codes[:, P * g : P * g + P].bitcast(FP8X4),
                lhsT_scale=scales[:, P * g : P * g + P],
                rhs=v_codes[win][:, C * g : C * g + C].bitcast(FP8X4),
                rhs_scale=v_scales[win][:, C * g : C * g + C],
                start=(g == 0),
                stop=(g == 1),
            )

        def weighted_sum(t):
            o_tiles[t] = ps_m.tile([P, C], F32, name="o_ps", tag="misc")
            weighted_half(t, 0, o_tiles[t])
            weighted_half(t, 1, o_tiles[t])

        def finish(t, o_ps, on_vector):
            win, blk = divmod(t, NBLK)
            o_sb = work.tile([P, C], F32, name="o_sb", tag="o_sb", bufs=10)
            recip = recips[t // GROUP][:, t % GROUP : t % GROUP + 1]
            if on_vector:
                nc.vector.tensor_scalar(
                    out=o_sb[:], in0=o_ps[:, 0:C], scalar1=recip, scalar2=None, op0=ALU.mult
                )
            else:
                nc.scalar.activation(out=o_sb[:], in_=o_ps[:, 0:C], func=ACT.Copy, scale=recip)
            yq, xq = image_slab(win, blk // 2)
            nc.sync.dma_start(out=o_blk[0, yq, xq, blk % 2], in_=o_sb[:])


        def exponent_half(t, g):
            if g == 0:
                e_tiles[t] = work.tile([P, 2, 2, 16, 16], BF16, name="e_sb", tag="e_sb")
                halves[t] = stat.tile([P, 2], F32, name="half_sum", tag="half_sum")
            nc.scalar.activation(
                out=e_tiles[t][:, g].rearrange("p u r w -> p r u w"),
                in_=x_tiles[t][:, HALF * g : HALF * g + HALF].rearrange("p (r u w) -> p r u w", r=16, u=2, w=16),
                func=ACT.Exp,
                bias=negs[t][:, 0:1],
                scale=1.0,
                accum_out=halves[t][:, g : g + 1],
            )

        def join_sums(t):
            nc.vector.tensor_reduce(out=sum_column(t), in_=halves[t][:], axis=AX.X, op=ALU.add)

        def transpose_half(t, g):
            et_tiles[(t, g)] = spare_bank(g)
            for u in range(2):
                nc.tensor.transpose(
                    out=et_tiles[(t, g)][:, P * u : P * u + P],
                    in_=e_tiles[t][:, g, u].rearrange("p r w -> p (r w)").bitcast(F32),
                    identity=ident_f[:],
                )

        def regroup_half(t, g, on_vector):
            if g == 0:
                g_tiles[t] = work.tile([P, 2, P, 4], BF16, name="grouped", tag="grouped", bufs=4, align_bytes=64)
            move_words(
                g_tiles[t][:, g].rearrange("p q j -> p (q j)").bitcast(F32).rearrange("p (q u) -> p q u", u=2),
                et_tiles[(t, g)][:, 0 : 2 * P].rearrange("p (u q) -> p q u", u=2),
                on_vector,
            )

        def quantise_half(t, g):
            if g == 0:
                codes = work.tile([P, 2 * P], U32, name="codes", tag="codes", bufs=5, align_bytes=64)
                scales = work.tile([P, 2 * P], U8, name="scales", tag="scales", bufs=5, align_bytes=64)
                c_tiles[t] = (codes, scales)
            codes, scales = c_tiles[t]
            nc.vector.quantize_mx(
                out=codes[:, P * g : P * g + P].bitcast(FP8X4),
                scales=scales[:, P * g : P * g + P],
                in_=g_tiles[t][:, g].rearrange("p q j -> p (q j)"),
            )

        def spare_bank(h):
            return ps_s.tile([P, HALF], F32, name="s_ps%d" % h, tag="s_ps%d" % h)

        def weighted_in(t, bank):
            o_tiles[t] = bank
            weighted_half(t, 0, bank)
            weighted_half(t, 1, bank)

        def valid(t):
            return 0 <= t < NT

        idle_passes(11)
        bank = transpose_blocks(k_sb, 0, [0, 1], ps_m, "misc")
        keep_k_slab(0, 0, 0, bank, True)
        bank = transpose_blocks(k_sb, 0, [2, 3], ps_m, "misc")
        keep_k_slab(0, 0, 1, bank, False)
        bank = transpose_blocks(q_sb, 0, [0], ps_e, "e_t")
        keep_q(0, [0], bank, True)
        bank = transpose_blocks(k_sb, 0, [4, 5], ps_e, "e_t")
        keep_k_slab(0, 1, 0, bank, False)
        bank = transpose_blocks(k_sb, 0, [6, 7], ps_m, "misc")
        keep_k_slab(0, 1, 1, bank, True)
        bank = transpose_blocks(q_sb, 0, [1], ps_s, "s_ps1")
        keep_q(0, [1], bank, False)
        scores(0)
        scores(1)
        bank = transpose_blocks(q_sb, 0, [2, 3], ps_m, "misc")
        keep_q(0, [2, 3], bank, False)
        bank = transpose_blocks(q_sb, 0, [4, 5, 6, 7], ps_e, "e_t")
        keep_q(0, [4, 5, 6, 7], bank, False)

        for tau in range(NT):
            win, blk = divmod(tau, NBLK)
            nxt = win + 1
            prepare = nxt < NWIN
            part = blk - 2
            last = tau - LAG_FINISH

            load_round(ROUNDS_AHEAD + tau)
            if valid(last):
                finish(last, o_tiles[last], False)
            if valid(tau - LAG_EXP):
                exponent(tau - LAG_EXP)
            if tau in v_rounds:
                group_v(win, v_rounds.index(tau) % 2)
            if prepare and 1 <= part < 3:
                keep_k(nxt, part - 1, bank)
            if prepare and 3 <= part < 5:
                keep_q(nxt, group, bank, False)
            if valid(tau - LAG_TRANSPOSE):
                transpose_e(tau - LAG_TRANSPOSE)
            if not valid(tau + 2):
                idle_passes(14)
                weighted_sum(tau - LAG_MX)
            if tau == 0 or tau > LAG_QUANTISE:
                add_mask(tau, 0)
            add_mask(tau, 1)
            if valid(tau + 2):
                scores_half(tau + 2, 0)
                if valid(tau - LAG_MX):
                    weighted_sum(tau - LAG_MX)
                scores_half(tau + 2, 1)
            if prepare and 0 <= part < 4:
                group = [4 * (part % 2) + i for i in range(4)]
                bank = transpose_blocks(k_sb if part < 2 else q_sb, nxt, group, ps_m, "misc")
            if valid(tau - LAG_QUANTISE):
                quantise_e(tau - LAG_QUANTISE)
            if valid(tau - LAG_RECIPROCAL) and (tau - LAG_RECIPROCAL) % GROUP == 0:
                reciprocal((tau - LAG_RECIPROCAL) // GROUP)
            if blk == 5:
                quantise_v(win)
            if tau < LAG_QUANTISE:
                add_mask(tau + 1, 0)
            row_max(tau)
            if valid(tau - LAG_REGROUP):
                regroup(tau - LAG_REGROUP, False)

        finish(25, o_tiles[25], False)
        exponent_half(31, 0)
        exponent_half(31, 1)
        weighted_sum(26)
        transpose_e(30)
        quantise_e(27)
        regroup(29, True)
        weighted_sum(27)
        transpose_half(31, 0)
        quantise_e(28)
        regroup_half(31, 0, False)
        finish(26, o_tiles[26], False)
        regroup(30, True)
        transpose_half(31, 1)
        weighted_in(28, spare_bank(0))
        regroup_half(31, 1, False)
        quantise_e(29)
        join_sums(31)
        weighted_in(29, spare_bank(1))
        quantise_half(31, 0)
        reciprocal(7)
        finish(27, o_tiles[27], False)
        quantise_e(30)
        o_tiles[31] = ps_e.tile([P, HALF], F32, name="e_t", tag="e_t")
        weighted_half(31, 0, o_tiles[31])
        quantise_half(31, 1)
        weighted_in(30, ps_e.tile([P, HALF], F32, name="e_t", tag="e_t"))
        weighted_half(31, 1, o_tiles[31])
        finish(28, o_tiles[28], True)
        finish(29, o_tiles[29], False)
        finish(30, o_tiles[30], False)
        finish(31, o_tiles[31], True)
